import numpy as np
import ml_dtypes


def mxq(x, axis, fmt="e4m3"):
    dtype, down = {"e4m3": (ml_dtypes.float8_e4m3fn, 7), "e5m2": (ml_dtypes.float8_e5m2, 14)}[fmt]
    v = np.moveaxis(np.asarray(x, np.float32).astype(ml_dtypes.bfloat16).astype(np.float64), axis, -1)
    blocks = v.reshape(v.shape[:-1] + (-1, 32))
    amax = np.abs(blocks).max(-1, keepdims=True)
    byte = np.maximum(np.where(amax > 0, np.frexp(amax)[1] - 1 + 127, 0) - down, 1)
    scale = np.exp2(byte - 127.0)
    codes = (blocks / scale).astype(np.float32).astype(dtype).astype(np.float64)
    return np.moveaxis((codes * scale).reshape(v.shape), -1, axis)


WIDE = False


def mx_kscale(k):
    if not WIDE:
        return np.ones(k)
    levels = np.array([20, -20, 10, -10, 0])
    a = np.random.permutation(np.resize(levels, k // 512 * 4)).reshape(k // 512, 4)
    idx = np.arange(k)
    return np.exp2(a[idx // 512, idx % 128 // 32])


BF16 = ml_dtypes.bfloat16


def bf(x):
    return np.asarray(x, np.float32).astype(BF16)


def f64(x):
    return np.asarray(x).astype(np.float64)


N, CI, CO, H, W, KH, KW = 2, 512, 512, 32, 34, 3, 3
HO, WO = H - KH + 1, W - KW + 1
L = N * HO * WO
K = KH * KW * CI


def setup_inputs():
    u = np.unique(mx_kscale(K))
    s = u[((np.arange(CI) // 32) * (len(u) - 1)) % len(u)][None, :, None, None]
    x = np.random.standard_normal((N, CI, H, W)) * s
    go = np.random.standard_normal((N, CO, HO, WO)) / np.sqrt(L)
    g = np.random.standard_normal((CO, CI, KH, KW)) * np.exp2(np.random.randint(-12, 1, (CO, 1, 1, 1))) * 0.25 / s
    return {"input": bf(x), "grad_output": bf(go), "grad_out": bf(g)}


def reference(input, grad_output, grad_out):
    xq = mxq(f64(input), 1, "e4m3")
    gq = mxq(f64(grad_out), 1, "e5m2")
    a = gq.transpose(0, 2, 3, 1).reshape(CO, K)
    wins = np.stack([xq[:, :, i:i + HO, j:j + WO] for i in range(KH) for j in range(KW)], axis=0)
    b = wins.transpose(0, 2, 1, 3, 4).reshape(K, L)
    y = a @ b
    return np.ascontiguousarray(y.reshape(CO, N, HO, WO).transpose(1, 0, 2, 3))

@@ -1,0 +1,162 @@
+from contextlib import ExitStack
+
+import concourse.mybir as mybir
+from concourse.masks import make_identity
+
+BF16 = mybir.dt.bfloat16
+F32 = mybir.dt.float32
+U32 = mybir.dt.uint32
+U8 = mybir.dt.uint8
+E4M3_X4 = mybir.dt.float8_e4m3fn_x4
+E5M2_X4 = mybir.dt.float8_e5m2_x4
+
+N_IMG, CI, CO, H, W, KH, KW = 2, 512, 512, 32, 34, 3, 3
+HO, WO = H - KH + 1, W - KW + 1
+TAPS = KH * KW
+
+P = 128
+PACK = 4
+O_TILES = CO // P
+ROWS = 8
+ROW_COLS = N_IMG * WO
+N_COLS = ROWS * ROW_COLS
+PIXEL_TILES = (HO + ROWS - 1) // ROWS
+X_CHUNKS = H // ROWS
+G_ROW = CI * TAPS
+WORDS = PACK * TAPS // 2
+TAP_PAIRS = (TAPS + 1) // 2
+
+FLOPS = 2 * CO * CI * TAPS * N_IMG * HO * WO
+BYTES = 2 * N_IMG * CI * H * W + 2 * CO * CI * TAPS + 4 * N_IMG * CO * HO * WO
+
+
+def tile_model_pa_kernel(tc, x, grad_output, g, out):
+    nc = tc.nc
+    with ExitStack() as ctx:
+        keep = ctx.enter_context(tc.tile_pool(name="keep", bufs=1))
+        x_stage = ctx.enter_context(tc.tile_pool(name="x_stage", bufs=6))
+        g_stage = ctx.enter_context(tc.tile_pool(name="g_stage", bufs=4))
+        out_stage = ctx.enter_context(tc.tile_pool(name="out_stage", bufs=4))
+        flip_banks = ctx.enter_context(tc.psum_pool(name="flip_banks", bufs=4))
+        sum_banks = ctx.enter_context(tc.psum_pool(name="sum_banks", bufs=4))
+
+        x_raw = keep.tile([P, N_IMG, PACK, H, W], BF16)
+        g_raw = keep.tile([P, O_TILES, G_ROW], BF16)
+        g_left = keep.tile([P, O_TILES, G_ROW], BF16)
+        identity = keep.tile([P, P], F32)
+        x_codes = keep.tile([P, KW, H * ROW_COLS], U32, align_bytes=64)
+        x_scales = keep.tile([P, KW, H * ROW_COLS], U8, align_bytes=64)
+        g_codes = keep.tile([P, O_TILES, TAPS, P], U32, align_bytes=64)
+        g_scales = keep.tile([P, O_TILES, TAPS, P], U8, align_bytes=64)
+
+        make_identity(nc, identity[:])
+        nc.vector.memset(g_left[:, :, G_ROW - 16 : G_ROW], 0.0)
+
+        def load_x_rows(first, count):
+            for n in range(N_IMG):
+                nc.sync.dma_start(
+                    out=x_raw[:, n, :, first : first + count, :].rearrange("p t r c -> p t (r c)"),
+                    in_=x[n, :, first : first + count, :].rearrange("(p t) r c -> p t (r c)", t=PACK),
+                )
+
+        g_rows = g.rearrange("o c kh kw -> o (c kh kw)")
+
+        def load_g_tile(a):
+            o_rows = slice(a * P, (a + 1) * P)
+            nc.sync.dma_start(out=g_raw[:, a, :], in_=g_rows[o_rows, :])
+            nc.sync.dma_start(out=g_left[:, a, 0 : G_ROW - 1], in_=g_rows[o_rows, 1:G_ROW])
+
+        load_x_rows(0, H // 2)
+        load_g_tile(0)
+        load_x_rows(H // 2, H // 2)
+        for a in range(1, O_TILES):
+            load_g_tile(a)
+
+        def prepare_x_rows(chunk):
+            rows = slice(chunk * ROWS, (chunk + 1) * ROWS)
+            cols = slice(chunk * N_COLS, (chunk + 1) * N_COLS)
+            grouped = []
+            for kw in range(KW):
+                x_grouped = x_stage.tile([P, ROWS, N_IMG, WO, PACK], BF16, align_bytes=64)
+                copy = nc.scalar.copy if kw == 1 else nc.vector.tensor_copy
+                for n in range(N_IMG):
+                    copy(
+                        out=x_grouped[:, :, n, :, :],
+                        in_=x_raw[:, n, :, rows, kw : kw + WO].rearrange("p t r j -> p r j t"),
+                    )
+                grouped.append(x_grouped)
+            for kw in range(KW):
+                nc.vector.quantize_mx(
+                    out=x_codes[:, kw, cols].bitcast(E4M3_X4),
+                    scales=x_scales[:, kw, cols],
+                    in_=grouped[kw][:].rearrange("p r n j t -> p (r n j t)"),
+                )
+
+        def prepare_g_tile(a):
+            words_of_even = g_raw[:, a, :].bitcast(F32).rearrange("o (p w) -> o w p", w=WORDS)
+            words_of_odd = g_left[:, a, :].bitcast(F32).rearrange("o (p w) -> o w p", w=WORDS)
+            for pair in range(TAP_PAIRS):
+                flipped = flip_banks.tile([P, PACK, P], F32)
+                for t in range(PACK):
+                    first_word = (t * TAPS) // 2
+                    words = words_of_even if t % 2 == 0 else words_of_odd
+                    nc.tensor.transpose(flipped[:, t, :], words[:, first_word + pair, :], identity[:])
+                taps = min(2, TAPS - 2 * pair)
+                g_grouped = g_stage.tile([P, 2, P, PACK], BF16, align_bytes=64)
+                copy = nc.scalar.copy if pair % 2 == 0 else nc.vector.tensor_copy
+                copy(
+                    out=g_grouped[:, 0:taps, :, :],
+                    in_=flipped[:].bitcast(BF16).rearrange("p t (o h) -> p h o t", h=2)[:, 0:taps, :, :],
+                )
+                tap_range = slice(2 * pair, 2 * pair + taps)
+                nc.vector.quantize_mx(
+                    out=g_codes[:, a, tap_range, :].rearrange("p k o -> p (k o)").bitcast(E5M2_X4),
+                    scales=g_scales[:, a, tap_range, :].rearrange("p k o -> p (k o)"),
+                    in_=g_grouped[:, 0:taps, :, :].rearrange("p k o t -> p (k o t)"),
+                )
+
+        def multiply(a, b):
+            first_row = min(b * ROWS, HO - ROWS)
+            sums = sum_banks.tile([P, N_COLS], F32)
+            for kh in range(KH):
+                for kw in range(KW):
+                    tap = kh * KW + kw
+                    cols = slice((first_row + kh) * ROW_COLS, (first_row + kh) * ROW_COLS + N_COLS)
+                    nc.tensor.matmul_mx(
+                        out=sums[:],
+                        lhsT=g_codes[:, a, tap, :].bitcast(E5M2_X4),
+                        lhsT_scale=g_scales[:, a, tap, :],
+                        rhs=x_codes[:, kw, cols].bitcast(E4M3_X4),
+                        rhs_scale=x_scales[:, kw, cols],
+                        start=(tap == 0),
+                        stop=(tap == TAPS - 1),
+                    )
+            skip = b * ROWS - first_row
+            fresh = ROWS - skip
+            result = out_stage.tile([P, N_IMG, ROWS, WO], F32)
+            nc.scalar.copy(
+                out=result[:, :, 0:fresh, :],
+                in_=sums[:].rearrange("p (i n j) -> p n i j", n=N_IMG, j=WO)[:, :, skip:ROWS, :],
+            )
+            nc.sync.dma_start(
+                out=out[:, a * P : (a + 1) * P, b * ROWS : b * ROWS + fresh, :].rearrange(
+                    "n o i j -> o n (i j)"
+                ),
+                in_=result[:, :, 0:fresh, :].rearrange("p n i j -> p n (i j)"),
+            )
+
+        prepare_x_rows(0)
+        prepare_x_rows(1)
+        ready_pixel_tiles = [0]
+        for a in range(O_TILES):
+            prepare_g_tile(a)
+            for b in ready_pixel_tiles:
+                multiply(a, b)
+            chunk = a + 2
+            if chunk < X_CHUNKS:
+                prepare_x_rows(chunk)
+                new_tiles = [chunk - 1] if chunk < X_CHUNKS - 1 else [chunk - 1, chunk]
+                for b in new_tiles:
+                    for earlier in range(a + 1):
+                        multiply(earlier, b)
+                ready_pixel_tiles.extend(new_tiles)

@@ -16,12 +16,12 @@ TAPS = KH * KW
 
 P = 128
 PACK = 4
-O_TILES = CO // P
+STEPS = CO // P
 ROWS = 8
 ROW_COLS = N_IMG * WO
 N_COLS = ROWS * ROW_COLS
-PIXEL_TILES = (HO + ROWS - 1) // ROWS
-X_CHUNKS = H // ROWS
+BAND = ROWS + KH - 1
+QUANT_ROWS = 2
 G_ROW = CI * TAPS
 WORDS = PACK * TAPS // 2
 TAP_PAIRS = (TAPS + 1) // 2
@@ -30,67 +30,76 @@ FLOPS = 2 * CO * CI * TAPS * N_IMG * HO * WO
 BYTES = 2 * N_IMG * CI * H * W + 2 * CO * CI * TAPS + 4 * N_IMG * CO * HO * WO
 
 
+def first_output_row(b):
+    return min(b * ROWS, HO - ROWS)
+
+
+def band_rows(b):
+    first = 0 if b == 0 else first_output_row(b - 1) + BAND
+    return first, first_output_row(b) + BAND
+
+
 def tile_model_pa_kernel(tc, x, grad_output, g, out):
     nc = tc.nc
     with ExitStack() as ctx:
         keep = ctx.enter_context(tc.tile_pool(name="keep", bufs=1))
-        x_stage = ctx.enter_context(tc.tile_pool(name="x_stage", bufs=6))
-        g_stage = ctx.enter_context(tc.tile_pool(name="g_stage", bufs=4))
+        x_stage = ctx.enter_context(tc.tile_pool(name="x_stage", bufs=2 * KW))
+        g_stage = ctx.enter_context(tc.tile_pool(name="g_stage", bufs=TAP_PAIRS))
         out_stage = ctx.enter_context(tc.tile_pool(name="out_stage", bufs=4))
         flip_banks = ctx.enter_context(tc.psum_pool(name="flip_banks", bufs=4))
         sum_banks = ctx.enter_context(tc.psum_pool(name="sum_banks", bufs=4))
 
-        x_raw = keep.tile([P, N_IMG, PACK, H, W], BF16)
-        g_raw = keep.tile([P, O_TILES, G_ROW], BF16)
-        g_left = keep.tile([P, O_TILES, G_ROW], BF16)
+        x_bands = [
+            keep.tile([P, N_IMG, PACK, BAND, W], BF16, name="x_band%d" % s) for s in range(STEPS)
+        ]
+        g_raw = keep.tile([P, STEPS, G_ROW], BF16)
+        g_left = keep.tile([P, STEPS, G_ROW], BF16)
         identity = keep.tile([P, P], F32)
         x_codes = keep.tile([P, KW, H * ROW_COLS], U32, align_bytes=64)
         x_scales = keep.tile([P, KW, H * ROW_COLS], U8, align_bytes=64)
-        g_codes = keep.tile([P, O_TILES, TAPS, P], U32, align_bytes=64)
-        g_scales = keep.tile([P, O_TILES, TAPS, P], U8, align_bytes=64)
+        g_codes = keep.tile([P, STEPS, TAPS, P], U32, align_bytes=64)
+        g_scales = keep.tile([P, STEPS, TAPS, P], U8, align_bytes=64)
 
         make_identity(nc, identity[:])
         nc.vector.memset(g_left[:, :, G_ROW - 16 : G_ROW], 0.0)
 
-        def load_x_rows(first, count):
+        g_rows = g.rearrange("o c kh kw -> o (c kh kw)")
+        for s in range(STEPS):
+            first, end = band_rows(s)
             for n in range(N_IMG):
                 nc.sync.dma_start(
-                    out=x_raw[:, n, :, first : first + count, :].rearrange("p t r c -> p t (r c)"),
-                    in_=x[n, :, first : first + count, :].rearrange("(p t) r c -> p t (r c)", t=PACK),
+                    out=x_bands[s][:, n, :, 0 : end - first, :].rearrange("p t r c -> p t (r c)"),
+                    in_=x[n, :, first:end, :].rearrange("(p t) r c -> p t (r c)", t=PACK),
                 )
+            o_rows = slice(s * P, (s + 1) * P)
+            nc.sync.dma_start(out=g_raw[:, s, :], in_=g_rows[o_rows, :])
+            nc.sync.dma_start(out=g_left[:, s, 0 : G_ROW - 1], in_=g_rows[o_rows, 1:G_ROW])
 
-        g_rows = g.rearrange("o c kh kw -> o (c kh kw)")
-
-        def load_g_tile(a):
-            o_rows = slice(a * P, (a + 1) * P)
-            nc.sync.dma_start(out=g_raw[:, a, :], in_=g_rows[o_rows, :])
-            nc.sync.dma_start(out=g_left[:, a, 0 : G_ROW - 1], in_=g_rows[o_rows, 1:G_ROW])
-
-        load_x_rows(0, H // 2)
-        load_g_tile(0)
-        load_x_rows(H // 2, H // 2)
-        for a in range(1, O_TILES):
-            load_g_tile(a)
-
-        def prepare_x_rows(chunk):
-            rows = slice(chunk * ROWS, (chunk + 1) * ROWS)
-            cols = slice(chunk * N_COLS, (chunk + 1) * N_COLS)
+        def prepare_x_band(b):
+            first, end = band_rows(b)
+            count = end - first
             grouped = []
             for kw in range(KW):
-                x_grouped = x_stage.tile([P, ROWS, N_IMG, WO, PACK], BF16, align_bytes=64)
-                copy = nc.scalar.copy if kw == 1 else nc.vector.tensor_copy
+                x_grouped = x_stage.tile([P, BAND, N_IMG, WO, PACK], BF16, align_bytes=64)
                 for n in range(N_IMG):
-                    copy(
-                        out=x_grouped[:, :, n, :, :],
-                        in_=x_raw[:, n, :, rows, kw : kw + WO].rearrange("p t r j -> p r j t"),
-                    )
+                    src = x_bands[b][:, n, :, 0:count, kw : kw + WO]
+                    dst = x_grouped[:, 0:count, n, :, :]
+                    if kw == 1:
+                        nc.scalar.copy(out=dst, in_=src.rearrange("p t r j -> p r j t"))
+                    else:
+                        nc.vector.tensor_copy(
+                            out=dst.rearrange("p r (c i) t -> p r c t i", i=4),
+                            in_=src.rearrange("p t r (c i) -> p r c t i", i=4),
+                        )
                 grouped.append(x_grouped)
-            for kw in range(KW):
-                nc.vector.quantize_mx(
-                    out=x_codes[:, kw, cols].bitcast(E4M3_X4),
-                    scales=x_scales[:, kw, cols],
-                    in_=grouped[kw][:].rearrange("p r n j t -> p (r n j t)"),
-                )
+            for r in range(0, count, QUANT_ROWS):
+                cols = slice((first + r) * ROW_COLS, (first + r + QUANT_ROWS) * ROW_COLS)
+                for kw in range(KW):
+                    nc.vector.quantize_mx(
+                        out=x_codes[:, kw, cols].bitcast(E4M3_X4),
+                        scales=x_scales[:, kw, cols],
+                        in_=grouped[kw][:, r : r + QUANT_ROWS].rearrange("p r n j t -> p (r n j t)"),
+                    )
 
         def prepare_g_tile(a):
             words_of_even = g_raw[:, a, :].bitcast(F32).rearrange("o (p w) -> o w p", w=WORDS)
@@ -116,7 +125,7 @@ def tile_model_pa_kernel(tc, x, grad_output, g, out):
                 )
 
         def multiply(a, b):
-            first_row = min(b * ROWS, HO - ROWS)
+            first_row = first_output_row(b)
             sums = sum_banks.tile([P, N_COLS], F32)
             for kh in range(KH):
                 for kw in range(KW):
@@ -145,18 +154,13 @@ def tile_model_pa_kernel(tc, x, grad_output, g, out):
                 in_=result[:, :, 0:fresh, :].rearrange("p n i j -> p n (i j)"),
             )
 
-        prepare_x_rows(0)
-        prepare_x_rows(1)
-        ready_pixel_tiles = [0]
-        for a in range(O_TILES):
-            prepare_g_tile(a)
-            for b in ready_pixel_tiles:
-                multiply(a, b)
-            chunk = a + 2
-            if chunk < X_CHUNKS:
-                prepare_x_rows(chunk)
-                new_tiles = [chunk - 1] if chunk < X_CHUNKS - 1 else [chunk - 1, chunk]
-                for b in new_tiles:
-                    for earlier in range(a + 1):
-                        multiply(earlier, b)
-                ready_pixel_tiles.extend(new_tiles)
+        ctx.enter_context(tc.manual_schedule())
+        prepare_x_band(0)
+        for s in range(STEPS):
+            prepare_g_tile(s)
+            if s + 1 < STEPS:
+                prepare_x_band(s + 1)
+            for a in range(s):
+                multiply(a, s)
+            for b in range(s + 1):
+                multiply(s, b)

@@ -25,6 +25,9 @@ QUANT_ROWS = 2
 G_ROW = CI * TAPS
 WORDS = PACK * TAPS // 2
 TAP_PAIRS = (TAPS + 1) // 2
+FLIPPED = 2
+PIECE = PACK * TAPS
+PIECE_PITCH = 48
 
 FLOPS = 2 * CO * CI * TAPS * N_IMG * HO * WO
 BYTES = 2 * N_IMG * CI * H * W + 2 * CO * CI * TAPS + 4 * N_IMG * CO * HO * WO
@@ -52,8 +55,9 @@ def tile_model_pa_kernel(tc, x, grad_output, g, out):
         x_bands = [
             keep.tile([P, N_IMG, PACK, BAND, W], BF16, name="x_band%d" % s) for s in range(STEPS)
         ]
-        g_raw = keep.tile([P, STEPS, G_ROW], BF16)
-        g_left = keep.tile([P, STEPS, G_ROW], BF16)
+        g_raw = keep.tile([P, FLIPPED, G_ROW], BF16)
+        g_left = keep.tile([P, FLIPPED, G_ROW], BF16)
+        g_pieces = keep.tile([P, STEPS - FLIPPED, P, PIECE_PITCH], BF16)
         identity = keep.tile([P, P], F32)
         x_codes = keep.tile([P, KW, H * ROW_COLS], U32, align_bytes=64)
         x_scales = keep.tile([P, KW, H * ROW_COLS], U8, align_bytes=64)
@@ -71,9 +75,15 @@ def tile_model_pa_kernel(tc, x, grad_output, g, out):
                     out=x_bands[s][:, n, :, 0 : end - first, :].rearrange("p t r c -> p t (r c)"),
                     in_=x[n, :, first:end, :].rearrange("(p t) r c -> p t (r c)", t=PACK),
                 )
-            o_rows = slice(s * P, (s + 1) * P)
-            nc.sync.dma_start(out=g_raw[:, s, :], in_=g_rows[o_rows, :])
-            nc.sync.dma_start(out=g_left[:, s, 0 : G_ROW - 1], in_=g_rows[o_rows, 1:G_ROW])
+            if s < FLIPPED:
+                o_rows = slice(s * P, (s + 1) * P)
+                nc.sync.dma_start(out=g_raw[:, s, :], in_=g_rows[o_rows, :])
+                nc.sync.dma_start(out=g_left[:, s, 0 : G_ROW - 1], in_=g_rows[o_rows, 1:G_ROW])
+        for a in range(FLIPPED, STEPS):
+            nc.sync.dma_start(
+                out=g_pieces[:, a - FLIPPED, :, 0:PIECE],
+                in_=g_rows[a * P : (a + 1) * P, :].rearrange("o (p e) -> p o e", e=PIECE),
+            )
 
         def prepare_x_band(b):
             first, end = band_rows(b)
@@ -101,7 +111,25 @@ def tile_model_pa_kernel(tc, x, grad_output, g, out):
                         in_=grouped[kw][:, r : r + QUANT_ROWS].rearrange("p r n j t -> p (r n j t)"),
                     )
 
-        def prepare_g_tile(a):
+        def quantise_g(a, pair, taps, g_grouped):
+            tap_range = slice(2 * pair, 2 * pair + taps)
+            nc.vector.quantize_mx(
+                out=g_codes[:, a, tap_range, :].rearrange("p k o -> p (k o)").bitcast(E5M2_X4),
+                scales=g_scales[:, a, tap_range, :].rearrange("p k o -> p (k o)"),
+                in_=g_grouped[:, 0:taps, :, :].rearrange("p k o t -> p (k o t)"),
+            )
+
+        def regroup_g_tile(a):
+            by_tap = g_pieces[:, a - FLIPPED, :, 0:PIECE].rearrange("p o (t k) -> p k o t", k=TAPS)
+            for pair in range(TAP_PAIRS):
+                taps = min(2, TAPS - 2 * pair)
+                g_grouped = g_stage.tile([P, 2, P, PACK], BF16, align_bytes=64)
+                nc.vector.tensor_copy(
+                    out=g_grouped[:, 0:taps, :, :], in_=by_tap[:, 2 * pair : 2 * pair + taps, :, :]
+                )
+                quantise_g(a, pair, taps, g_grouped)
+
+        def flip_g_tile(a):
             words_of_even = g_raw[:, a, :].bitcast(F32).rearrange("o (p w) -> o w p", w=WORDS)
             words_of_odd = g_left[:, a, :].bitcast(F32).rearrange("o (p w) -> o w p", w=WORDS)
             for pair in range(TAP_PAIRS):
@@ -117,12 +145,7 @@ def tile_model_pa_kernel(tc, x, grad_output, g, out):
                     out=g_grouped[:, 0:taps, :, :],
                     in_=flipped[:].bitcast(BF16).rearrange("p t (o h) -> p h o t", h=2)[:, 0:taps, :, :],
                 )
-                tap_range = slice(2 * pair, 2 * pair + taps)
-                nc.vector.quantize_mx(
-                    out=g_codes[:, a, tap_range, :].rearrange("p k o -> p (k o)").bitcast(E5M2_X4),
-                    scales=g_scales[:, a, tap_range, :].rearrange("p k o -> p (k o)"),
-                    in_=g_grouped[:, 0:taps, :, :].rearrange("p k o t -> p (k o t)"),
-                )
+                quantise_g(a, pair, taps, g_grouped)
 
         def multiply(a, b):
             first_row = first_output_row(b)
@@ -147,7 +170,7 @@ def tile_model_pa_kernel(tc, x, grad_output, g, out):
                 out=result[:, :, 0:fresh, :],
                 in_=sums[:].rearrange("p (i n j) -> p n i j", n=N_IMG, j=WO)[:, :, skip:ROWS, :],
             )
-            nc.sync.dma_start(
+            nc.scalar.dma_start(
                 out=out[:, a * P : (a + 1) * P, b * ROWS : b * ROWS + fresh, :].rearrange(
                     "n o i j -> o n (i j)"
                 ),
@@ -157,10 +180,16 @@ def tile_model_pa_kernel(tc, x, grad_output, g, out):
         ctx.enter_context(tc.manual_schedule())
         prepare_x_band(0)
         for s in range(STEPS):
-            prepare_g_tile(s)
+            if s < FLIPPED:
+                flip_g_tile(s)
             if s + 1 < STEPS:
                 prepare_x_band(s + 1)
-            for a in range(s):
+            for a in range(min(s, FLIPPED)):
                 multiply(a, s)
-            for b in range(s + 1):
-                multiply(s, b)
+            if s < FLIPPED:
+                for b in range(s + 1):
+                    multiply(s, b)
+        for a in range(FLIPPED, STEPS):
+            regroup_g_tile(a)
+            for b in range(STEPS):
+                multiply(a, b)

@@ -25,9 +25,6 @@ QUANT_ROWS = 2
 G_ROW = CI * TAPS
 WORDS = PACK * TAPS // 2
 TAP_PAIRS = (TAPS + 1) // 2
-FLIPPED = 2
-PIECE = PACK * TAPS
-PIECE_PITCH = 48
 
 FLOPS = 2 * CO * CI * TAPS * N_IMG * HO * WO
 BYTES = 2 * N_IMG * CI * H * W + 2 * CO * CI * TAPS + 4 * N_IMG * CO * HO * WO
@@ -49,15 +46,14 @@ def tile_model_pa_kernel(tc, x, grad_output, g, out):
         x_stage = ctx.enter_context(tc.tile_pool(name="x_stage", bufs=2 * KW))
         g_stage = ctx.enter_context(tc.tile_pool(name="g_stage", bufs=TAP_PAIRS))
         out_stage = ctx.enter_context(tc.tile_pool(name="out_stage", bufs=4))
-        flip_banks = ctx.enter_context(tc.psum_pool(name="flip_banks", bufs=4))
-        sum_banks = ctx.enter_context(tc.psum_pool(name="sum_banks", bufs=4))
+        flip_banks = ctx.enter_context(tc.psum_pool(name="flip_banks", bufs=TAP_PAIRS))
+        sum_banks = ctx.enter_context(tc.psum_pool(name="sum_banks", bufs=8 - TAP_PAIRS))
 
         x_bands = [
             keep.tile([P, N_IMG, PACK, BAND, W], BF16, name="x_band%d" % s) for s in range(STEPS)
         ]
-        g_raw = keep.tile([P, FLIPPED, G_ROW], BF16)
-        g_left = keep.tile([P, FLIPPED, G_ROW], BF16)
-        g_pieces = keep.tile([P, STEPS - FLIPPED, P, PIECE_PITCH], BF16)
+        g_raw = keep.tile([P, STEPS, G_ROW], BF16)
+        g_left = keep.tile([P, STEPS, G_ROW], BF16)
         identity = keep.tile([P, P], F32)
         x_codes = keep.tile([P, KW, H * ROW_COLS], U32, align_bytes=64)
         x_scales = keep.tile([P, KW, H * ROW_COLS], U8, align_bytes=64)
@@ -75,15 +71,9 @@ def tile_model_pa_kernel(tc, x, grad_output, g, out):
                     out=x_bands[s][:, n, :, 0 : end - first, :].rearrange("p t r c -> p t (r c)"),
                     in_=x[n, :, first:end, :].rearrange("(p t) r c -> p t (r c)", t=PACK),
                 )
-            if s < FLIPPED:
-                o_rows = slice(s * P, (s + 1) * P)
-                nc.sync.dma_start(out=g_raw[:, s, :], in_=g_rows[o_rows, :])
-                nc.sync.dma_start(out=g_left[:, s, 0 : G_ROW - 1], in_=g_rows[o_rows, 1:G_ROW])
-        for a in range(FLIPPED, STEPS):
-            nc.sync.dma_start(
-                out=g_pieces[:, a - FLIPPED, :, 0:PIECE],
-                in_=g_rows[a * P : (a + 1) * P, :].rearrange("o (p e) -> p o e", e=PIECE),
-            )
+            o_rows = slice(s * P, (s + 1) * P)
+            nc.sync.dma_start(out=g_raw[:, s, :], in_=g_rows[o_rows, :])
+            nc.sync.dma_start(out=g_left[:, s, 0 : G_ROW - 1], in_=g_rows[o_rows, 1:G_ROW])
 
         def prepare_x_band(b):
             first, end = band_rows(b)
@@ -111,41 +101,32 @@ def tile_model_pa_kernel(tc, x, grad_output, g, out):
                         in_=grouped[kw][:, r : r + QUANT_ROWS].rearrange("p r n j t -> p (r n j t)"),
                     )
 
-        def quantise_g(a, pair, taps, g_grouped):
-            tap_range = slice(2 * pair, 2 * pair + taps)
-            nc.vector.quantize_mx(
-                out=g_codes[:, a, tap_range, :].rearrange("p k o -> p (k o)").bitcast(E5M2_X4),
-                scales=g_scales[:, a, tap_range, :].rearrange("p k o -> p (k o)"),
-                in_=g_grouped[:, 0:taps, :, :].rearrange("p k o t -> p (k o t)"),
-            )
-
-        def regroup_g_tile(a):
-            by_tap = g_pieces[:, a - FLIPPED, :, 0:PIECE].rearrange("p o (t k) -> p k o t", k=TAPS)
+        def flip_channels(a, parity, banks):
+            source = g_raw if parity == 0 else g_left
+            words = source[:, a, :].bitcast(F32).rearrange("o (p w) -> o w p", w=WORDS)
             for pair in range(TAP_PAIRS):
-                taps = min(2, TAPS - 2 * pair)
-                g_grouped = g_stage.tile([P, 2, P, PACK], BF16, align_bytes=64)
-                nc.vector.tensor_copy(
-                    out=g_grouped[:, 0:taps, :, :], in_=by_tap[:, 2 * pair : 2 * pair + taps, :, :]
-                )
-                quantise_g(a, pair, taps, g_grouped)
-
-        def flip_g_tile(a):
-            words_of_even = g_raw[:, a, :].bitcast(F32).rearrange("o (p w) -> o w p", w=WORDS)
-            words_of_odd = g_left[:, a, :].bitcast(F32).rearrange("o (p w) -> o w p", w=WORDS)
-            for pair in range(TAP_PAIRS):
-                flipped = flip_banks.tile([P, PACK, P], F32)
-                for t in range(PACK):
+                for t in range(parity, PACK, 2):
                     first_word = (t * TAPS) // 2
-                    words = words_of_even if t % 2 == 0 else words_of_odd
-                    nc.tensor.transpose(flipped[:, t, :], words[:, first_word + pair, :], identity[:])
+                    nc.tensor.transpose(banks[pair][:, t, :], words[:, first_word + pair, :], identity[:])
+
+        def quantise_g_tile(a, banks):
+            for pair in range(TAP_PAIRS):
                 taps = min(2, TAPS - 2 * pair)
                 g_grouped = g_stage.tile([P, 2, P, PACK], BF16, align_bytes=64)
                 copy = nc.scalar.copy if pair % 2 == 0 else nc.vector.tensor_copy
                 copy(
                     out=g_grouped[:, 0:taps, :, :],
-                    in_=flipped[:].bitcast(BF16).rearrange("p t (o h) -> p h o t", h=2)[:, 0:taps, :, :],
+                    in_=banks[pair][:].bitcast(BF16).rearrange("p t (o h) -> p h o t", h=2)[:, 0:taps, :, :],
                 )
-                quantise_g(a, pair, taps, g_grouped)
+                tap_range = slice(2 * pair, 2 * pair + taps)
+                nc.vector.quantize_mx(
+                    out=g_codes[:, a, tap_range, :].rearrange("p k o -> p (k o)").bitcast(E5M2_X4),
+                    scales=g_scales[:, a, tap_range, :].rearrange("p k o -> p (k o)"),
+                    in_=g_grouped[:, 0:taps, :, :].rearrange("p k o t -> p (k o t)"),
+                )
+
+        def new_banks():
+            return [flip_banks.tile([P, PACK, P], F32, name="flipped") for pair in range(TAP_PAIRS)]
 
         def multiply(a, b):
             first_row = first_output_row(b)
@@ -170,7 +151,7 @@ def tile_model_pa_kernel(tc, x, grad_output, g, out):
                 out=result[:, :, 0:fresh, :],
                 in_=sums[:].rearrange("p (i n j) -> p n i j", n=N_IMG, j=WO)[:, :, skip:ROWS, :],
             )
-            nc.scalar.dma_start(
+            nc.sync.dma_start(
                 out=out[:, a * P : (a + 1) * P, b * ROWS : b * ROWS + fresh, :].rearrange(
                     "n o i j -> o n (i j)"
                 ),
@@ -179,17 +160,23 @@ def tile_model_pa_kernel(tc, x, grad_output, g, out):
 
         ctx.enter_context(tc.manual_schedule())
         prepare_x_band(0)
+        banks = new_banks()
+        flip_channels(0, 0, banks)
+        flip_channels(0, 1, banks)
+        quantise_g_tile(0, banks)
         for s in range(STEPS):
-            if s < FLIPPED:
-                flip_g_tile(s)
-            if s + 1 < STEPS:
+            products = [(a, s) for a in range(s)] + [(s, b) for b in range(s + 1)]
+            if s + 1 == STEPS:
+                for a, b in products:
+                    multiply(a, b)
+            else:
                 prepare_x_band(s + 1)
-            for a in range(min(s, FLIPPED)):
-                multiply(a, s)
-            if s < FLIPPED:
-                for b in range(s + 1):
-                    multiply(s, b)
-        for a in range(FLIPPED, STEPS):
-            regroup_g_tile(a)
-            for b in range(STEPS):
-                multiply(a, b)
+                banks = new_banks()
+                multiply(products[0][0], products[0][1])
+                flip_channels(s + 1, 0, banks)
+                for a, b in products[1:2]:
+                    multiply(a, b)
+                flip_channels(s + 1, 1, banks)
+                quantise_g_tile(s + 1, banks)
+                for a, b in products[2:]:
+                    multiply(a, b)

@@ -25,6 +25,9 @@ QUANT_ROWS = 2
 G_ROW = CI * TAPS
 WORDS = PACK * TAPS // 2
 TAP_PAIRS = (TAPS + 1) // 2
+FLIPPED = 3
+PIECE = PACK * TAPS
+PIECE_PITCH = 48
 
 FLOPS = 2 * CO * CI * TAPS * N_IMG * HO * WO
 BYTES = 2 * N_IMG * CI * H * W + 2 * CO * CI * TAPS + 4 * N_IMG * CO * HO * WO
@@ -52,8 +55,9 @@ def tile_model_pa_kernel(tc, x, grad_output, g, out):
         x_bands = [
             keep.tile([P, N_IMG, PACK, BAND, W], BF16, name="x_band%d" % s) for s in range(STEPS)
         ]
-        g_raw = keep.tile([P, STEPS, G_ROW], BF16)
-        g_left = keep.tile([P, STEPS, G_ROW], BF16)
+        g_raw = keep.tile([P, FLIPPED, G_ROW], BF16)
+        g_left = keep.tile([P, FLIPPED, G_ROW], BF16)
+        g_pieces = keep.tile([P, STEPS - FLIPPED, P, PIECE_PITCH], BF16)
         identity = keep.tile([P, P], F32)
         x_codes = keep.tile([P, KW, H * ROW_COLS], U32, align_bytes=64)
         x_scales = keep.tile([P, KW, H * ROW_COLS], U8, align_bytes=64)
@@ -71,9 +75,15 @@ def tile_model_pa_kernel(tc, x, grad_output, g, out):
                     out=x_bands[s][:, n, :, 0 : end - first, :].rearrange("p t r c -> p t (r c)"),
                     in_=x[n, :, first:end, :].rearrange("(p t) r c -> p t (r c)", t=PACK),
                 )
-            o_rows = slice(s * P, (s + 1) * P)
-            nc.sync.dma_start(out=g_raw[:, s, :], in_=g_rows[o_rows, :])
-            nc.sync.dma_start(out=g_left[:, s, 0 : G_ROW - 1], in_=g_rows[o_rows, 1:G_ROW])
+            if s < FLIPPED:
+                o_rows = slice(s * P, (s + 1) * P)
+                nc.sync.dma_start(out=g_raw[:, s, :], in_=g_rows[o_rows, :])
+                nc.sync.dma_start(out=g_left[:, s, 0 : G_ROW - 1], in_=g_rows[o_rows, 1:G_ROW])
+        for a in range(FLIPPED, STEPS):
+            nc.sync.dma_start(
+                out=g_pieces[:, a - FLIPPED, :, 0:PIECE],
+                in_=g_rows[a * P : (a + 1) * P, :].rearrange("o (p e) -> p o e", e=PIECE),
+            )
 
         def prepare_x_band(b):
             first, end = band_rows(b)
@@ -109,21 +119,27 @@ def tile_model_pa_kernel(tc, x, grad_output, g, out):
                     first_word = (t * TAPS) // 2
                     nc.tensor.transpose(banks[pair][:, t, :], words[:, first_word + pair, :], identity[:])
 
-        def quantise_g_tile(a, banks):
+        def quantise_g_taps(a, pair, copy, by_tap):
+            taps = min(2, TAPS - 2 * pair)
+            g_grouped = g_stage.tile([P, 2, P, PACK], BF16, align_bytes=64)
+            copy(out=g_grouped[:, 0:taps, :, :], in_=by_tap[:, 0:taps, :, :])
+            tap_range = slice(2 * pair, 2 * pair + taps)
+            nc.vector.quantize_mx(
+                out=g_codes[:, a, tap_range, :].rearrange("p k o -> p (k o)").bitcast(E5M2_X4),
+                scales=g_scales[:, a, tap_range, :].rearrange("p k o -> p (k o)"),
+                in_=g_grouped[:, 0:taps, :, :].rearrange("p k o t -> p (k o t)"),
+            )
+
+        def quantise_flipped_tile(a, banks):
             for pair in range(TAP_PAIRS):
-                taps = min(2, TAPS - 2 * pair)
-                g_grouped = g_stage.tile([P, 2, P, PACK], BF16, align_bytes=64)
                 copy = nc.scalar.copy if pair % 2 == 0 else nc.vector.tensor_copy
-                copy(
-                    out=g_grouped[:, 0:taps, :, :],
-                    in_=banks[pair][:].bitcast(BF16).rearrange("p t (o h) -> p h o t", h=2)[:, 0:taps, :, :],
-                )
-                tap_range = slice(2 * pair, 2 * pair + taps)
-                nc.vector.quantize_mx(
-                    out=g_codes[:, a, tap_range, :].rearrange("p k o -> p (k o)").bitcast(E5M2_X4),
-                    scales=g_scales[:, a, tap_range, :].rearrange("p k o -> p (k o)"),
-                    in_=g_grouped[:, 0:taps, :, :].rearrange("p k o t -> p (k o t)"),
-                )
+                halves = banks[pair][:].bitcast(BF16).rearrange("p t (o h) -> p h o t", h=2)
+                quantise_g_taps(a, pair, copy, halves)
+
+        def quantise_tile_in_pieces(a):
+            by_tap = g_pieces[:, a - FLIPPED, :, 0:PIECE].rearrange("p o (t k) -> p k o t", k=TAPS)
+            for pair in range(TAP_PAIRS):
+                quantise_g_taps(a, pair, nc.vector.tensor_copy, by_tap[:, 2 * pair : TAPS, :, :])
 
         def new_banks():
             return [flip_banks.tile([P, PACK, P], F32, name="flipped") for pair in range(TAP_PAIRS)]
@@ -151,7 +167,7 @@ def tile_model_pa_kernel(tc, x, grad_output, g, out):
                 out=result[:, :, 0:fresh, :],
                 in_=sums[:].rearrange("p (i n j) -> p n i j", n=N_IMG, j=WO)[:, :, skip:ROWS, :],
             )
-            nc.sync.dma_start(
+            nc.scalar.dma_start(
                 out=out[:, a * P : (a + 1) * P, b * ROWS : b * ROWS + fresh, :].rearrange(
                     "n o i j -> o n (i j)"
                 ),
@@ -163,20 +179,22 @@ def tile_model_pa_kernel(tc, x, grad_output, g, out):
         banks = new_banks()
         flip_channels(0, 0, banks)
         flip_channels(0, 1, banks)
-        quantise_g_tile(0, banks)
+        quantise_flipped_tile(0, banks)
         for s in range(STEPS):
             products = [(a, s) for a in range(s)] + [(s, b) for b in range(s + 1)]
-            if s + 1 == STEPS:
-                for a, b in products:
-                    multiply(a, b)
-            else:
+            if s + 1 < STEPS:
                 prepare_x_band(s + 1)
+            if s + 1 < FLIPPED:
                 banks = new_banks()
-                multiply(products[0][0], products[0][1])
+                for a, b in products[0:1]:
+                    multiply(a, b)
                 flip_channels(s + 1, 0, banks)
                 for a, b in products[1:2]:
                     multiply(a, b)
                 flip_channels(s + 1, 1, banks)
-                quantise_g_tile(s + 1, banks)
-                for a, b in products[2:]:
-                    multiply(a, b)
+                quantise_flipped_tile(s + 1, banks)
+                products = products[2:]
+            elif s + 1 < STEPS:
+                quantise_tile_in_pieces(s + 1)
+            for a, b in products:
+                multiply(a, b)

@@ -28,6 +28,7 @@ TAP_PAIRS = (TAPS + 1) // 2
 FLIPPED = 3
 PIECE = PACK * TAPS
 PIECE_PITCH = 48
+HALF = P // 2
 
 FLOPS = 2 * CO * CI * TAPS * N_IMG * HO * WO
 BYTES = 2 * N_IMG * CI * H * W + 2 * CO * CI * TAPS + 4 * N_IMG * CO * HO * WO
@@ -48,6 +49,7 @@ def tile_model_pa_kernel(tc, x, grad_output, g, out):
         keep = ctx.enter_context(tc.tile_pool(name="keep", bufs=1))
         x_stage = ctx.enter_context(tc.tile_pool(name="x_stage", bufs=2 * KW))
         g_stage = ctx.enter_context(tc.tile_pool(name="g_stage", bufs=TAP_PAIRS))
+        piece_stage = ctx.enter_context(tc.tile_pool(name="piece_stage", bufs=KH))
         out_stage = ctx.enter_context(tc.tile_pool(name="out_stage", bufs=4))
         flip_banks = ctx.enter_context(tc.psum_pool(name="flip_banks", bufs=TAP_PAIRS))
         sum_banks = ctx.enter_context(tc.psum_pool(name="sum_banks", bufs=8 - TAP_PAIRS))
@@ -57,7 +59,7 @@ def tile_model_pa_kernel(tc, x, grad_output, g, out):
         ]
         g_raw = keep.tile([P, FLIPPED, G_ROW], BF16)
         g_left = keep.tile([P, FLIPPED, G_ROW], BF16)
-        g_pieces = keep.tile([P, STEPS - FLIPPED, P, PIECE_PITCH], BF16)
+        g_pieces = keep.tile([P, P, PIECE_PITCH], BF16)
         identity = keep.tile([P, P], F32)
         x_codes = keep.tile([P, KW, H * ROW_COLS], U32, align_bytes=64)
         x_scales = keep.tile([P, KW, H * ROW_COLS], U8, align_bytes=64)
@@ -79,10 +81,11 @@ def tile_model_pa_kernel(tc, x, grad_output, g, out):
                 o_rows = slice(s * P, (s + 1) * P)
                 nc.sync.dma_start(out=g_raw[:, s, :], in_=g_rows[o_rows, :])
                 nc.sync.dma_start(out=g_left[:, s, 0 : G_ROW - 1], in_=g_rows[o_rows, 1:G_ROW])
-        for a in range(FLIPPED, STEPS):
+        for half in range(2):
+            first_o = FLIPPED * P + half * HALF
             nc.sync.dma_start(
-                out=g_pieces[:, a - FLIPPED, :, 0:PIECE],
-                in_=g_rows[a * P : (a + 1) * P, :].rearrange("o (p e) -> p o e", e=PIECE),
+                out=g_pieces[:, half * HALF : (half + 1) * HALF, 0:PIECE],
+                in_=g_rows[first_o : first_o + HALF, :].rearrange("o (p e) -> p o e", e=PIECE),
             )
 
         def prepare_x_band(b):
@@ -136,31 +139,39 @@ def tile_model_pa_kernel(tc, x, grad_output, g, out):
                 halves = banks[pair][:].bitcast(BF16).rearrange("p t (o h) -> p h o t", h=2)
                 quantise_g_taps(a, pair, copy, halves)
 
-        def quantise_tile_in_pieces(a):
-            by_tap = g_pieces[:, a - FLIPPED, :, 0:PIECE].rearrange("p o (t k) -> p k o t", k=TAPS)
-            for pair in range(TAP_PAIRS):
-                quantise_g_taps(a, pair, nc.vector.tensor_copy, by_tap[:, 2 * pair : TAPS, :, :])
+        def quantise_tile_in_pieces():
+            for half in range(2):
+                o_half = slice(half * HALF, (half + 1) * HALF)
+                by_tap = g_pieces[:, o_half, 0:PIECE].rearrange("p o (t k) -> p k o t", k=TAPS)
+                for kh in range(KH):
+                    piece_grouped = piece_stage.tile([P, KW, HALF, PACK], BF16, align_bytes=64)
+                    nc.vector.tensor_copy(out=piece_grouped[:], in_=by_tap[:, kh * KW : (kh + 1) * KW, :, :])
+                    for kw in range(KW):
+                        nc.vector.quantize_mx(
+                            out=g_codes[:, FLIPPED, kh * KW + kw, o_half].bitcast(E5M2_X4),
+                            scales=g_scales[:, FLIPPED, kh * KW + kw, o_half],
+                            in_=piece_grouped[:, kw, :, :].rearrange("p o t -> p (o t)"),
+                        )
 
         def new_banks():
             return [flip_banks.tile([P, PACK, P], F32, name="flipped") for pair in range(TAP_PAIRS)]
 
-        def multiply(a, b):
-            first_row = first_output_row(b)
-            sums = sum_banks.tile([P, N_COLS], F32)
-            for kh in range(KH):
-                for kw in range(KW):
-                    tap = kh * KW + kw
-                    cols = slice((first_row + kh) * ROW_COLS, (first_row + kh) * ROW_COLS + N_COLS)
-                    nc.tensor.matmul_mx(
-                        out=sums[:],
-                        lhsT=g_codes[:, a, tap, :].bitcast(E5M2_X4),
-                        lhsT_scale=g_scales[:, a, tap, :],
-                        rhs=x_codes[:, kw, cols].bitcast(E4M3_X4),
-                        rhs_scale=x_scales[:, kw, cols],
-                        start=(tap == 0),
-                        stop=(tap == TAPS - 1),
-                    )
-            skip = b * ROWS - first_row
+        def one_pass(a, b, tap, sums):
+            kh, kw = divmod(tap, KW)
+            first_col = (first_output_row(b) + kh) * ROW_COLS
+            cols = slice(first_col, first_col + N_COLS)
+            nc.tensor.matmul_mx(
+                out=sums[:],
+                lhsT=g_codes[:, a, tap, :].bitcast(E5M2_X4),
+                lhsT_scale=g_scales[:, a, tap, :],
+                rhs=x_codes[:, kw, cols].bitcast(E4M3_X4),
+                rhs_scale=x_scales[:, kw, cols],
+                start=(tap == 0),
+                stop=(tap == TAPS - 1),
+            )
+
+        def store_product(a, b, sums):
+            skip = b * ROWS - first_output_row(b)
             fresh = ROWS - skip
             result = out_stage.tile([P, N_IMG, ROWS, WO], F32)
             nc.scalar.copy(
@@ -181,20 +192,23 @@ def tile_model_pa_kernel(tc, x, grad_output, g, out):
         flip_channels(0, 1, banks)
         quantise_flipped_tile(0, banks)
         for s in range(STEPS):
-            products = [(a, s) for a in range(s)] + [(s, b) for b in range(s + 1)]
             if s + 1 < STEPS:
                 prepare_x_band(s + 1)
             if s + 1 < FLIPPED:
                 banks = new_banks()
-                for a, b in products[0:1]:
-                    multiply(a, b)
-                flip_channels(s + 1, 0, banks)
-                for a, b in products[1:2]:
-                    multiply(a, b)
-                flip_channels(s + 1, 1, banks)
-                quantise_flipped_tile(s + 1, banks)
-                products = products[2:]
             elif s + 1 < STEPS:
-                quantise_tile_in_pieces(s + 1)
+                quantise_tile_in_pieces()
+            products = [(a, s) for a in range(s)] + [(s, b) for b in range(s + 1)]
+            third = len(products) * TAPS // 3
+            done = 0
             for a, b in products:
-                multiply(a, b)
+                sums = sum_banks.tile([P, N_COLS], F32)
+                for tap in range(TAPS):
+                    one_pass(a, b, tap, sums)
+                    done += 1
+                    if s + 1 < FLIPPED and done == third:
+                        flip_channels(s + 1, 0, banks)
+                    if s + 1 < FLIPPED and done == 2 * third:
+                        flip_channels(s + 1, 1, banks)
+                        quantise_flipped_tile(s + 1, banks)
+                store_product(a, b, sums)

@@ -21,7 +21,7 @@ ROWS = 8
 ROW_COLS = N_IMG * WO
 N_COLS = ROWS * ROW_COLS
 BAND = ROWS + KH - 1
-QUANT_ROWS = 2
+QUANT_ROWS = 8
 G_ROW = CI * TAPS
 WORDS = PACK * TAPS // 2
 TAP_PAIRS = (TAPS + 1) // 2
@@ -88,31 +88,37 @@ def tile_model_pa_kernel(tc, x, grad_output, g, out):
                 in_=g_rows[first_o : first_o + HALF, :].rearrange("o (p e) -> p o e", e=PIECE),
             )
 
-        def prepare_x_band(b):
+        def group_x(b, kw):
             first, end = band_rows(b)
             count = end - first
-            grouped = []
-            for kw in range(KW):
-                x_grouped = x_stage.tile([P, BAND, N_IMG, WO, PACK], BF16, align_bytes=64)
-                for n in range(N_IMG):
-                    src = x_bands[b][:, n, :, 0:count, kw : kw + WO]
-                    dst = x_grouped[:, 0:count, n, :, :]
-                    if kw == 1:
-                        nc.scalar.copy(out=dst, in_=src.rearrange("p t r j -> p r j t"))
-                    else:
-                        nc.vector.tensor_copy(
-                            out=dst.rearrange("p r (c i) t -> p r c t i", i=4),
-                            in_=src.rearrange("p t r (c i) -> p r c t i", i=4),
-                        )
-                grouped.append(x_grouped)
-            for r in range(0, count, QUANT_ROWS):
-                cols = slice((first + r) * ROW_COLS, (first + r + QUANT_ROWS) * ROW_COLS)
-                for kw in range(KW):
-                    nc.vector.quantize_mx(
-                        out=x_codes[:, kw, cols].bitcast(E4M3_X4),
-                        scales=x_scales[:, kw, cols],
-                        in_=grouped[kw][:, r : r + QUANT_ROWS].rearrange("p r n j t -> p (r n j t)"),
+            x_grouped = x_stage.tile([P, BAND, N_IMG, WO, PACK], BF16, align_bytes=64)
+            for n in range(N_IMG):
+                src = x_bands[b][:, n, :, 0:count, kw : kw + WO]
+                dst = x_grouped[:, 0:count, n, :, :]
+                if kw == 1:
+                    nc.scalar.copy(out=dst, in_=src.rearrange("p t r j -> p r j t"))
+                else:
+                    nc.vector.tensor_copy(
+                        out=dst.rearrange("p r (c i) t -> p r c t i", i=4),
+                        in_=src.rearrange("p t r (c i) -> p r c t i", i=4),
                     )
+            return x_grouped
+
+        def quantise_x(b, kw, x_grouped):
+            first, end = band_rows(b)
+            count = end - first
+            r = 0
+            while r < count:
+                rows = QUANT_ROWS
+                while rows > count - r:
+                    rows //= 2
+                cols = slice((first + r) * ROW_COLS, (first + r + rows) * ROW_COLS)
+                nc.vector.quantize_mx(
+                    out=x_codes[:, kw, cols].bitcast(E4M3_X4),
+                    scales=x_scales[:, kw, cols],
+                    in_=x_grouped[:, r : r + rows].rearrange("p r n j t -> p (r n j t)"),
+                )
+                r += rows
 
         def flip_channels(a, parity, banks):
             source = g_raw if parity == 0 else g_left
@@ -122,10 +128,16 @@ def tile_model_pa_kernel(tc, x, grad_output, g, out):
                     first_word = (t * TAPS) // 2
                     nc.tensor.transpose(banks[pair][:, t, :], words[:, first_word + pair, :], identity[:])
 
-        def quantise_g_taps(a, pair, copy, by_tap):
+        def empty_bank(pair, banks):
             taps = min(2, TAPS - 2 * pair)
+            copy = nc.vector.tensor_copy if pair == 1 else nc.scalar.copy
             g_grouped = g_stage.tile([P, 2, P, PACK], BF16, align_bytes=64)
-            copy(out=g_grouped[:, 0:taps, :, :], in_=by_tap[:, 0:taps, :, :])
+            halves = banks[pair][:].bitcast(BF16).rearrange("p t (o h) -> p h o t", h=2)
+            copy(out=g_grouped[:, 0:taps, :, :], in_=halves[:, 0:taps, :, :])
+            return g_grouped
+
+        def quantise_taps(a, pair, g_grouped):
+            taps = min(2, TAPS - 2 * pair)
             tap_range = slice(2 * pair, 2 * pair + taps)
             nc.vector.quantize_mx(
                 out=g_codes[:, a, tap_range, :].rearrange("p k o -> p (k o)").bitcast(E5M2_X4),
@@ -133,11 +145,24 @@ def tile_model_pa_kernel(tc, x, grad_output, g, out):
                 in_=g_grouped[:, 0:taps, :, :].rearrange("p k o t -> p (k o t)"),
             )
 
-        def quantise_flipped_tile(a, banks):
-            for pair in range(TAP_PAIRS):
-                copy = nc.scalar.copy if pair % 2 == 0 else nc.vector.tensor_copy
-                halves = banks[pair][:].bitcast(BF16).rearrange("p t (o h) -> p h o t", h=2)
-                quantise_g_taps(a, pair, copy, halves)
+        def finish_tile_and_band(a, banks, b):
+            g0 = empty_bank(0, banks)
+            g1 = empty_bank(1, banks)
+            quantise_taps(a, 0, g0)
+            quantise_taps(a, 1, g1)
+            g2 = empty_bank(2, banks)
+            x0 = group_x(b, 0) if b is not None else None
+            quantise_taps(a, 2, g2)
+            g3 = empty_bank(3, banks)
+            x2 = group_x(b, 2) if b is not None else None
+            quantise_taps(a, 3, g3)
+            g4 = empty_bank(4, banks)
+            quantise_taps(a, 4, g4)
+            if b is not None:
+                x1 = group_x(b, 1)
+                quantise_x(b, 0, x0)
+                quantise_x(b, 2, x2)
+                quantise_x(b, 1, x1)
 
         def quantise_tile_in_pieces():
             for half in range(2):
@@ -156,7 +181,7 @@ def tile_model_pa_kernel(tc, x, grad_output, g, out):
         def new_banks():
             return [flip_banks.tile([P, PACK, P], F32, name="flipped") for pair in range(TAP_PAIRS)]
 
-        def one_pass(a, b, tap, sums):
+        def one_pass(a, b, tap, sums, start, stop):
             kh, kw = divmod(tap, KW)
             first_col = (first_output_row(b) + kh) * ROW_COLS
             cols = slice(first_col, first_col + N_COLS)
@@ -166,8 +191,8 @@ def tile_model_pa_kernel(tc, x, grad_output, g, out):
                 lhsT_scale=g_scales[:, a, tap, :],
                 rhs=x_codes[:, kw, cols].bitcast(E4M3_X4),
                 rhs_scale=x_scales[:, kw, cols],
-                start=(tap == 0),
-                stop=(tap == TAPS - 1),
+                start=start,
+                stop=stop,
             )
 
         def store_product(a, b, sums):
@@ -186,29 +211,39 @@ def tile_model_pa_kernel(tc, x, grad_output, g, out):
             )
 
         ctx.enter_context(tc.manual_schedule())
-        prepare_x_band(0)
+        x0 = group_x(0, 0)
+        x1 = group_x(0, 1)
+        x2 = group_x(0, 2)
+        quantise_x(0, 0, x0)
+        quantise_x(0, 2, x2)
+        quantise_x(0, 1, x1)
         banks = new_banks()
         flip_channels(0, 0, banks)
         flip_channels(0, 1, banks)
-        quantise_flipped_tile(0, banks)
+        finish_tile_and_band(0, banks, 1)
+        by_kw = [kh * KW + kw for kw in (0, 2, 1) for kh in range(KH)]
         for s in range(STEPS):
-            if s + 1 < STEPS:
-                prepare_x_band(s + 1)
             if s + 1 < FLIPPED:
                 banks = new_banks()
             elif s + 1 < STEPS:
                 quantise_tile_in_pieces()
             products = [(a, s) for a in range(s)] + [(s, b) for b in range(s + 1)]
-            third = len(products) * TAPS // 3
+            passes = len(products) * TAPS
+            first_run = 4 if s == 0 else passes // 3
+            second_run = passes if s == 0 else 2 * passes // 3
             done = 0
-            for a, b in products:
+            for i, (a, b) in enumerate(products):
                 sums = sum_banks.tile([P, N_COLS], F32)
-                for tap in range(TAPS):
-                    one_pass(a, b, tap, sums)
+                order = by_kw if (i == 0 and s > 0) else list(range(TAPS))
+                flipped = False
+                for j, tap in enumerate(order):
+                    one_pass(a, b, tap, sums, j == 0, j == TAPS - 1)
                     done += 1
-                    if s + 1 < FLIPPED and done == third:
+                    if s + 1 < FLIPPED and done == first_run:
                         flip_channels(s + 1, 0, banks)
-                    if s + 1 < FLIPPED and done == 2 * third:
+                    if s + 1 < FLIPPED and done == second_run:
                         flip_channels(s + 1, 1, banks)
-                        quantise_flipped_tile(s + 1, banks)
+                        flipped = True
                 store_product(a, b, sums)
+                if flipped:
+                    finish_tile_and_band(s + 1, banks, s + 2 if s + 2 < STEPS else None)

@@ -96,12 +96,13 @@ def tile_model_pa_kernel(tc, x, grad_output, g, out):
                 src = x_bands[b][:, n, :, 0:count, kw : kw + WO]
                 dst = x_grouped[:, 0:count, n, :, :]
                 if kw == 1:
-                    nc.scalar.copy(out=dst, in_=src.rearrange("p t r j -> p r j t"))
+                    copy = nc.scalar.copy
                 else:
-                    nc.vector.tensor_copy(
-                        out=dst.rearrange("p r (c i) t -> p r c t i", i=4),
-                        in_=src.rearrange("p t r (c i) -> p r c t i", i=4),
-                    )
+                    copy = nc.vector.tensor_copy
+                copy(
+                    out=dst.rearrange("p r (c i) t -> p r c t i", i=4),
+                    in_=src.rearrange("p t r (c i) -> p r c t i", i=4),
+                )
             return x_grouped
 
         def quantise_x(b, kw, x_grouped):
@@ -170,7 +171,10 @@ def tile_model_pa_kernel(tc, x, grad_output, g, out):
                 by_tap = g_pieces[:, o_half, 0:PIECE].rearrange("p o (t k) -> p k o t", k=TAPS)
                 for kh in range(KH):
                     piece_grouped = piece_stage.tile([P, KW, HALF, PACK], BF16, align_bytes=64)
-                    nc.vector.tensor_copy(out=piece_grouped[:], in_=by_tap[:, kh * KW : (kh + 1) * KW, :, :])
+                    nc.vector.tensor_copy(
+                        out=piece_grouped[:].rearrange("p k o t -> p o t k"),
+                        in_=by_tap[:, kh * KW : (kh + 1) * KW, :, :].rearrange("p k o t -> p o t k"),
+                    )
                     for kw in range(KW):
                         nc.vector.quantize_mx(
                             out=g_codes[:, FLIPPED, kh * KW + kw, o_half].bitcast(E5M2_X4),

@@ -68,6 +68,8 @@ def tile_model_pa_kernel(tc, x, grad_output, g, out):
 
         make_identity(nc, identity[:])
         nc.vector.memset(g_left[:, :, G_ROW - 16 : G_ROW], 0.0)
+        odd_left = g_left[:, 0, G_ROW // 2 : G_ROW].rearrange("o (q e) -> o q e", e=2 * TAPS)
+        nc.vector.memset(odd_left[:, :, 2 * TAPS - 2 : 2 * TAPS], 0.0)
 
         g_rows = g.rearrange("o c kh kw -> o (c kh kw)")
         for s in range(STEPS):
@@ -80,7 +82,8 @@ def tile_model_pa_kernel(tc, x, grad_output, g, out):
             if s < FLIPPED:
                 o_rows = slice(s * P, (s + 1) * P)
                 nc.sync.dma_start(out=g_raw[:, s, :], in_=g_rows[o_rows, :])
-                nc.sync.dma_start(out=g_left[:, s, 0 : G_ROW - 1], in_=g_rows[o_rows, 1:G_ROW])
+                left_end = G_ROW // 2 if s == 0 else G_ROW - 1
+                nc.sync.dma_start(out=g_left[:, s, 0:left_end], in_=g_rows[o_rows, 1 : left_end + 1])
         for half in range(2):
             first_o = FLIPPED * P + half * HALF
             nc.sync.dma_start(
@@ -128,6 +131,10 @@ def tile_model_pa_kernel(tc, x, grad_output, g, out):
                 for t in range(parity, PACK, 2):
                     first_word = (t * TAPS) // 2
                     nc.tensor.transpose(banks[pair][:, t, :], words[:, first_word + pair, :], identity[:])
+
+        def shift_odd_channels():
+            odd_raw = g_raw[:, 0, G_ROW // 2 : G_ROW].rearrange("o (q e) -> o q e", e=2 * TAPS)
+            nc.scalar.copy(out=odd_left[:, :, TAPS - 1 : 2 * TAPS - 1], in_=odd_raw[:, :, TAPS : 2 * TAPS])
 
         def empty_bank(pair, banks):
             taps = min(2, TAPS - 2 * pair)
@@ -222,6 +229,7 @@ def tile_model_pa_kernel(tc, x, grad_output, g, out):
         quantise_x(0, 2, x2)
         quantise_x(0, 1, x1)
         banks = new_banks()
+        shift_odd_channels()
         flip_channels(0, 0, banks)
         flip_channels(0, 1, banks)
         finish_tile_and_band(0, banks, 1)

@@ -26,6 +26,9 @@ G_ROW = CI * TAPS
 WORDS = PACK * TAPS // 2
 TAP_PAIRS = (TAPS + 1) // 2
 FLIPPED = 3
+SHIFTED = 2
+HALVES = PACK // 2
+RUN = 4
 PIECE = PACK * TAPS
 PIECE_PITCH = 48
 HALF = P // 2
@@ -58,7 +61,8 @@ def tile_model_pa_kernel(tc, x, grad_output, g, out):
             keep.tile([P, N_IMG, PACK, BAND, W], BF16, name="x_band%d" % s) for s in range(STEPS)
         ]
         g_raw = keep.tile([P, FLIPPED, G_ROW], BF16)
-        g_left = keep.tile([P, FLIPPED, G_ROW], BF16)
+        g_left = keep.tile([P, SHIFTED, G_ROW], BF16)
+        g_ordered = keep.tile([P, TAPS, HALVES, P, 2], BF16)
         g_pieces = keep.tile([P, P, PIECE_PITCH], BF16)
         identity = keep.tile([P, P], F32)
         x_codes = keep.tile([P, KW, H * ROW_COLS], U32, align_bytes=64)
@@ -72,18 +76,28 @@ def tile_model_pa_kernel(tc, x, grad_output, g, out):
         nc.vector.memset(odd_left[:, :, 2 * TAPS - 2 : 2 * TAPS], 0.0)
 
         g_rows = g.rearrange("o c kh kw -> o (c kh kw)")
-        for s in range(STEPS):
+        def load_band(s):
             first, end = band_rows(s)
             for n in range(N_IMG):
                 nc.sync.dma_start(
                     out=x_bands[s][:, n, :, 0 : end - first, :].rearrange("p t r c -> p t (r c)"),
                     in_=x[n, :, first:end, :].rearrange("(p t) r c -> p t (r c)", t=PACK),
                 )
-            if s < FLIPPED:
-                o_rows = slice(s * P, (s + 1) * P)
-                nc.sync.dma_start(out=g_raw[:, s, :], in_=g_rows[o_rows, :])
+
+        def load_tile(s):
+            o_rows = slice(s * P, (s + 1) * P)
+            nc.sync.dma_start(out=g_raw[:, s, :], in_=g_rows[o_rows, :])
+            if s < SHIFTED:
                 left_end = G_ROW // 2 if s == 0 else G_ROW - 1
                 nc.sync.dma_start(out=g_left[:, s, 0:left_end], in_=g_rows[o_rows, 1 : left_end + 1])
+
+        load_band(0)
+        load_tile(0)
+        load_band(1)
+        load_tile(1)
+        load_band(2)
+        load_band(3)
+        load_tile(2)
         for half in range(2):
             first_o = FLIPPED * P + half * HALF
             nc.sync.dma_start(
@@ -131,6 +145,29 @@ def tile_model_pa_kernel(tc, x, grad_output, g, out):
                 for t in range(parity, PACK, 2):
                     first_word = (t * TAPS) // 2
                     nc.tensor.transpose(banks[pair][:, t, :], words[:, first_word + pair, :], identity[:])
+
+        def order_tile():
+            by_tap = g_raw[:, SHIFTED, :].rearrange("o (p u e k) -> o u p e k", u=HALVES, e=2, k=TAPS)
+            for first_tap in range(0, TAPS, RUN):
+                taps = slice(first_tap, min(first_tap + RUN, TAPS))
+                nc.vector.tensor_copy(
+                    out=g_ordered[:, taps, :, :, :].rearrange("o k u p e -> o u p e k"),
+                    in_=by_tap[:, :, :, :, taps],
+                )
+
+        def flip_ordered_tile(banks):
+            for tap in range(TAPS):
+                for u in range(HALVES):
+                    words = g_ordered[:, tap, u, :, :].rearrange("o p e -> o (p e)").bitcast(F32)
+                    nc.tensor.transpose(banks[tap // 2][:, (tap % 2) * HALVES + u, :], words, identity[:])
+
+        def finish_ordered_tile(banks):
+            for pair in range(TAP_PAIRS):
+                taps = min(2, TAPS - 2 * pair)
+                g_grouped = g_stage.tile([P, 2, P, PACK], BF16, align_bytes=64)
+                by_word = banks[pair][:].rearrange("p (k u) o -> p k o u", u=HALVES)
+                nc.scalar.copy(out=g_grouped[:, 0:taps, :, :].bitcast(F32), in_=by_word[:, 0:taps, :, :])
+                quantise_taps(SHIFTED, pair, g_grouped)
 
         def shift_odd_channels():
             odd_raw = g_raw[:, 0, G_ROW // 2 : G_ROW].rearrange("o (q e) -> o q e", e=2 * TAPS)
@@ -234,28 +271,33 @@ def tile_model_pa_kernel(tc, x, grad_output, g, out):
         flip_channels(0, 1, banks)
         finish_tile_and_band(0, banks, 1)
         by_kw = [kh * KW + kw for kw in (0, 2, 1) for kh in range(KH)]
-        for s in range(STEPS):
-            if s + 1 < FLIPPED:
+        sequence = [(0, 0), (0, 1), (1, 0), (1, 1), (0, 2), (1, 2), (0, 3), (1, 3)]
+        sequence += [(a, b) for a in range(SHIFTED, STEPS) for b in range(STEPS)]
+        for i, (a, b) in enumerate(sequence):
+            if i == 0:
                 banks = new_banks()
-            elif s + 1 < STEPS:
+            sums = sum_banks.tile([P, N_COLS], F32)
+            order = by_kw if (a == 0 and b > 0) else list(range(TAPS))
+            for j, tap in enumerate(order):
+                one_pass(a, b, tap, sums, j == 0, j == TAPS - 1)
+                if i == 0 and j == 3:
+                    flip_channels(1, 0, banks)
+            if i == 0:
+                flip_channels(1, 1, banks)
+            if (a, b) == (1, 2):
+                banks = new_banks()
+                flip_ordered_tile(banks)
+            store_product(a, b, sums)
+            if i == 0:
+                finish_tile_and_band(1, banks, 2)
+            if i == 1:
+                x0 = group_x(3, 0)
+                x1 = group_x(3, 1)
+                x2 = group_x(3, 2)
+                quantise_x(3, 0, x0)
+                quantise_x(3, 2, x2)
+                quantise_x(3, 1, x1)
+                order_tile()
+            if (a, b) == (1, 2):
+                finish_ordered_tile(banks)
                 quantise_tile_in_pieces()
-            products = [(a, s) for a in range(s)] + [(s, b) for b in range(s + 1)]
-            passes = len(products) * TAPS
-            first_run = 4 if s == 0 else passes // 3
-            second_run = passes if s == 0 else 2 * passes // 3
-            done = 0
-            for i, (a, b) in enumerate(products):
-                sums = sum_banks.tile([P, N_COLS], F32)
-                order = by_kw if (i == 0 and s > 0) else list(range(TAPS))
-                flipped = False
-                for j, tap in enumerate(order):
-                    one_pass(a, b, tap, sums, j == 0, j == TAPS - 1)
-                    done += 1
-                    if s + 1 < FLIPPED and done == first_run:
-                        flip_channels(s + 1, 0, banks)
-                    if s + 1 < FLIPPED and done == second_run:
-                        flip_channels(s + 1, 1, banks)
-                        flipped = True
-                store_product(a, b, sums)
-                if flipped:
-                    finish_tile_and_band(s + 1, banks, s + 2 if s + 2 < STEPS else None)

@@ -190,24 +190,28 @@ def tile_model_pa_kernel(tc, x, grad_output, g, out):
                 in_=g_grouped[:, 0:taps, :, :].rearrange("p k o t -> p (k o t)"),
             )
 
-        def finish_tile_and_band(a, banks, b):
+        def finish_tile_and_band(a, banks, b, between):
             g0 = empty_bank(0, banks)
             g1 = empty_bank(1, banks)
             quantise_taps(a, 0, g0)
             quantise_taps(a, 1, g1)
             g2 = empty_bank(2, banks)
-            x0 = group_x(b, 0) if b is not None else None
+            if between:
+                x0 = group_x(b, 0)
             quantise_taps(a, 2, g2)
             g3 = empty_bank(3, banks)
-            x2 = group_x(b, 2) if b is not None else None
+            if between:
+                x2 = group_x(b, 2)
             quantise_taps(a, 3, g3)
             g4 = empty_bank(4, banks)
             quantise_taps(a, 4, g4)
-            if b is not None:
-                x1 = group_x(b, 1)
-                quantise_x(b, 0, x0)
-                quantise_x(b, 2, x2)
-                quantise_x(b, 1, x1)
+            if not between:
+                x0 = group_x(b, 0)
+                x2 = group_x(b, 2)
+            x1 = group_x(b, 1)
+            quantise_x(b, 0, x0)
+            quantise_x(b, 2, x2)
+            quantise_x(b, 1, x1)
 
         def quantise_tile_in_pieces():
             for half in range(2):
@@ -269,7 +273,7 @@ def tile_model_pa_kernel(tc, x, grad_output, g, out):
         shift_odd_channels()
         flip_channels(0, 0, banks)
         flip_channels(0, 1, banks)
-        finish_tile_and_band(0, banks, 1)
+        finish_tile_and_band(0, banks, 1, True)
         by_kw = [kh * KW + kw for kw in (0, 2, 1) for kh in range(KH)]
         sequence = [(0, 0), (0, 1), (1, 0), (1, 1), (0, 2), (1, 2), (0, 3), (1, 3)]
         sequence += [(a, b) for a in range(SHIFTED, STEPS) for b in range(STEPS)]
@@ -284,12 +288,12 @@ def tile_model_pa_kernel(tc, x, grad_output, g, out):
                     flip_channels(1, 0, banks)
             if i == 0:
                 flip_channels(1, 1, banks)
-            if (a, b) == (1, 2):
+            if (a, b) == (0, 3):
                 banks = new_banks()
                 flip_ordered_tile(banks)
             store_product(a, b, sums)
             if i == 0:
-                finish_tile_and_band(1, banks, 2)
+                finish_tile_and_band(1, banks, 2, False)
             if i == 1:
                 x0 = group_x(3, 0)
                 x1 = group_x(3, 1)
@@ -298,6 +302,6 @@ def tile_model_pa_kernel(tc, x, grad_output, g, out):
                 quantise_x(3, 2, x2)
                 quantise_x(3, 1, x1)
                 order_tile()
-            if (a, b) == (1, 2):
+            if (a, b) == (0, 3):
                 finish_ordered_tile(banks)
                 quantise_tile_in_pieces()

@@ -7,6 +7,7 @@ BF16 = mybir.dt.bfloat16
 F32 = mybir.dt.float32
 U32 = mybir.dt.uint32
 U8 = mybir.dt.uint8
+I32 = mybir.dt.int32
 E4M3_X4 = mybir.dt.float8_e4m3fn_x4
 E5M2_X4 = mybir.dt.float8_e5m2_x4
 
@@ -21,6 +22,8 @@ ROWS = 8
 ROW_COLS = N_IMG * WO
 N_COLS = ROWS * ROW_COLS
 BAND = ROWS + KH - 1
+EXTRA = W - WO
+EXTRA_PIXELS = 64
 QUANT_ROWS = 8
 G_ROW = CI * TAPS
 WORDS = PACK * TAPS // 2
@@ -67,10 +70,14 @@ def tile_model_pa_kernel(tc, x, grad_output, g, out):
         identity = keep.tile([P, P], F32)
         x_codes = keep.tile([P, KW, H * ROW_COLS], U32, align_bytes=64)
         x_scales = keep.tile([P, KW, H * ROW_COLS], U8, align_bytes=64)
+        x_extra = keep.tile([P, STEPS, EXTRA_PIXELS, PACK], BF16, align_bytes=64)
+        extra_codes = keep.tile([P, STEPS, EXTRA_PIXELS], U32, align_bytes=64)
+        extra_scales = keep.tile([P, STEPS, EXTRA_PIXELS], U8, align_bytes=64)
         g_codes = keep.tile([P, STEPS, TAPS, P], U32, align_bytes=64)
         g_scales = keep.tile([P, STEPS, TAPS, P], U8, align_bytes=64)
 
         make_identity(nc, identity[:])
+        nc.vector.memset(x_extra[:], 0.0)
         nc.vector.memset(g_left[:, :, G_ROW - 16 : G_ROW], 0.0)
         odd_left = g_left[:, 0, G_ROW // 2 : G_ROW].rearrange("o (q e) -> o q e", e=2 * TAPS)
         nc.vector.memset(odd_left[:, :, 2 * TAPS - 2 : 2 * TAPS], 0.0)
@@ -105,24 +112,26 @@ def tile_model_pa_kernel(tc, x, grad_output, g, out):
                 in_=g_rows[first_o : first_o + HALF, :].rearrange("o (p e) -> p o e", e=PIECE),
             )
 
-        def group_x(b, kw):
+        def group_image(b, n, x_grouped):
             first, end = band_rows(b)
             count = end - first
-            x_grouped = x_stage.tile([P, BAND, N_IMG, WO, PACK], BF16, align_bytes=64)
-            for n in range(N_IMG):
-                src = x_bands[b][:, n, :, 0:count, kw : kw + WO]
-                dst = x_grouped[:, 0:count, n, :, :]
-                if kw == 1:
-                    copy = nc.scalar.copy
-                else:
-                    copy = nc.vector.tensor_copy
-                copy(
-                    out=dst.rearrange("p r (c i) t -> p r c t i", i=4),
-                    in_=src.rearrange("p t r (c i) -> p r c t i", i=4),
-                )
-            return x_grouped
+            copy = nc.vector.tensor_copy if n == 0 else nc.scalar.copy
+            copy(
+                out=x_grouped[:, 0:count, n, :, :].rearrange("p r (c i) t -> p r c t i", i=4),
+                in_=x_bands[b][:, n, :, 0:count, 0:WO].rearrange("p t r (c i) -> p r c t i", i=4),
+            )
 
-        def quantise_x(b, kw, x_grouped):
+        def group_extra(b):
+            first, end = band_rows(b)
+            count = end - first
+            nc.vector.tensor_copy(
+                out=x_extra[:, b, 0 : count * N_IMG * EXTRA, :].rearrange(
+                    "p (r n c) t -> p r n c t", n=N_IMG, c=EXTRA
+                ),
+                in_=x_bands[b][:, :, :, 0:count, WO:W].rearrange("p n t r c -> p r n c t"),
+            )
+
+        def quantise_x(b, x_grouped):
             first, end = band_rows(b)
             count = end - first
             r = 0
@@ -132,11 +141,40 @@ def tile_model_pa_kernel(tc, x, grad_output, g, out):
                     rows //= 2
                 cols = slice((first + r) * ROW_COLS, (first + r + rows) * ROW_COLS)
                 nc.vector.quantize_mx(
-                    out=x_codes[:, kw, cols].bitcast(E4M3_X4),
-                    scales=x_scales[:, kw, cols],
+                    out=x_codes[:, 0, cols].bitcast(E4M3_X4),
+                    scales=x_scales[:, 0, cols],
                     in_=x_grouped[:, r : r + rows].rearrange("p r n j t -> p (r n j t)"),
                 )
                 r += rows
+            nc.vector.quantize_mx(
+                out=extra_codes[:, b, :].bitcast(E4M3_X4),
+                scales=extra_scales[:, b, :],
+                in_=x_extra[:, b, :, :].rearrange("p c t -> p (c t)"),
+            )
+
+        def move_x(b, kw):
+            first, end = band_rows(b)
+            cols = slice(first * ROW_COLS, end * ROW_COLS)
+            spare = slice(0, (end - first) * N_IMG * EXTRA)
+            views = [
+                (x_codes[:, 0, cols].bitcast(I32), x_codes[:, kw, cols].bitcast(I32), extra_codes[:, b, spare].bitcast(I32)),
+                (x_scales[:, 0, cols], x_scales[:, kw, cols], extra_scales[:, b, spare]),
+            ]
+            for whole, moved, extra in views:
+                whole = whole.rearrange("p (q j) -> p q j", j=WO)
+                moved = moved.rearrange("p (q j) -> p q j", j=WO)
+                extra = extra.rearrange("p (q c) -> p q c", c=EXTRA)
+                nc.vector.tensor_copy(out=moved[:, :, 0 : WO - kw], in_=whole[:, :, kw:WO])
+                nc.vector.tensor_copy(out=moved[:, :, WO - kw : WO], in_=extra[:, :, 0:kw])
+
+        def new_stage():
+            return x_stage.tile([P, BAND, N_IMG, WO, PACK], BF16, align_bytes=64, name="x_grouped")
+
+        def finish_band(b, x_grouped):
+            group_image(b, 1, x_grouped)
+            quantise_x(b, x_grouped)
+            move_x(b, 1)
+            move_x(b, 2)
 
         def flip_channels(a, parity, banks):
             source = g_raw if parity == 0 else g_left
@@ -196,22 +234,19 @@ def tile_model_pa_kernel(tc, x, grad_output, g, out):
             quantise_taps(a, 0, g0)
             quantise_taps(a, 1, g1)
             g2 = empty_bank(2, banks)
+            x_grouped = new_stage()
             if between:
-                x0 = group_x(b, 0)
+                group_image(b, 0, x_grouped)
+                group_extra(b)
             quantise_taps(a, 2, g2)
             g3 = empty_bank(3, banks)
-            if between:
-                x2 = group_x(b, 2)
             quantise_taps(a, 3, g3)
             g4 = empty_bank(4, banks)
             quantise_taps(a, 4, g4)
             if not between:
-                x0 = group_x(b, 0)
-                x2 = group_x(b, 2)
-            x1 = group_x(b, 1)
-            quantise_x(b, 0, x0)
-            quantise_x(b, 2, x2)
-            quantise_x(b, 1, x1)
+                group_image(b, 0, x_grouped)
+                group_extra(b)
+            finish_band(b, x_grouped)
 
         def quantise_tile_in_pieces():
             for half in range(2):
@@ -263,18 +298,16 @@ def tile_model_pa_kernel(tc, x, grad_output, g, out):
             )
 
         ctx.enter_context(tc.manual_schedule())
-        x0 = group_x(0, 0)
-        x1 = group_x(0, 1)
-        x2 = group_x(0, 2)
-        quantise_x(0, 0, x0)
-        quantise_x(0, 2, x2)
-        quantise_x(0, 1, x1)
+        x_grouped = new_stage()
+        group_image(0, 0, x_grouped)
+        group_extra(0)
+        finish_band(0, x_grouped)
         banks = new_banks()
         shift_odd_channels()
         flip_channels(0, 0, banks)
         flip_channels(0, 1, banks)
         finish_tile_and_band(0, banks, 1, True)
-        by_kw = [kh * KW + kw for kw in (0, 2, 1) for kh in range(KH)]
+        by_kw = [kh * KW + kw for kw in range(KW) for kh in range(KH)]
         sequence = [(0, 0), (0, 1), (1, 0), (1, 1), (0, 2), (1, 2), (0, 3), (1, 3)]
         sequence += [(a, b) for a in range(SHIFTED, STEPS) for b in range(STEPS)]
         for i, (a, b) in enumerate(sequence):
@@ -295,12 +328,10 @@ def tile_model_pa_kernel(tc, x, grad_output, g, out):
             if i == 0:
                 finish_tile_and_band(1, banks, 2, False)
             if i == 1:
-                x0 = group_x(3, 0)
-                x1 = group_x(3, 1)
-                x2 = group_x(3, 2)
-                quantise_x(3, 0, x0)
-                quantise_x(3, 2, x2)
-                quantise_x(3, 1, x1)
+                x_grouped = new_stage()
+                group_image(3, 0, x_grouped)
+                group_extra(3)
+                finish_band(3, x_grouped)
                 order_tile()
             if (a, b) == (0, 3):
                 finish_ordered_tile(banks)

@@ -79,8 +79,11 @@ def tile_model_pa_kernel(tc, x, grad_output, g, out):
         make_identity(nc, identity[:])
         nc.vector.memset(x_extra[:], 0.0)
         nc.vector.memset(g_left[:, :, G_ROW - 16 : G_ROW], 0.0)
-        odd_left = g_left[:, 0, G_ROW // 2 : G_ROW].rearrange("o (q e) -> o q e", e=2 * TAPS)
-        nc.vector.memset(odd_left[:, :, 2 * TAPS - 2 : 2 * TAPS], 0.0)
+        odd_left = [
+            g_left[:, a, G_ROW // 2 : G_ROW].rearrange("o (q e) -> o q e", e=2 * TAPS) for a in range(SHIFTED)
+        ]
+        for a in range(SHIFTED):
+            nc.vector.memset(odd_left[a][:, :, 2 * TAPS - 2 : 2 * TAPS], 0.0)
 
         g_rows = g.rearrange("o c kh kw -> o (c kh kw)")
         def load_band(s):
@@ -95,7 +98,7 @@ def tile_model_pa_kernel(tc, x, grad_output, g, out):
             o_rows = slice(s * P, (s + 1) * P)
             nc.sync.dma_start(out=g_raw[:, s, :], in_=g_rows[o_rows, :])
             if s < SHIFTED:
-                left_end = G_ROW // 2 if s == 0 else G_ROW - 1
+                left_end = G_ROW // 2
                 nc.sync.dma_start(out=g_left[:, s, 0:left_end], in_=g_rows[o_rows, 1 : left_end + 1])
 
         load_band(0)
@@ -112,10 +115,9 @@ def tile_model_pa_kernel(tc, x, grad_output, g, out):
                 in_=g_rows[first_o : first_o + HALF, :].rearrange("o (p e) -> p o e", e=PIECE),
             )
 
-        def group_image(b, n, x_grouped):
+        def group_image(b, n, x_grouped, copy):
             first, end = band_rows(b)
             count = end - first
-            copy = nc.vector.tensor_copy if n == 0 else nc.scalar.copy
             copy(
                 out=x_grouped[:, 0:count, n, :, :].rearrange("p r (c i) t -> p r c t i", i=4),
                 in_=x_bands[b][:, n, :, 0:count, 0:WO].rearrange("p t r (c i) -> p r c t i", i=4),
@@ -170,8 +172,8 @@ def tile_model_pa_kernel(tc, x, grad_output, g, out):
         def new_stage():
             return x_stage.tile([P, BAND, N_IMG, WO, PACK], BF16, align_bytes=64, name="x_grouped")
 
-        def finish_band(b, x_grouped):
-            group_image(b, 1, x_grouped)
+        def finish_band(b, x_grouped, copy):
+            group_image(b, 1, x_grouped, copy)
             quantise_x(b, x_grouped)
             move_x(b, 1)
             move_x(b, 2)
@@ -207,9 +209,9 @@ def tile_model_pa_kernel(tc, x, grad_output, g, out):
                 nc.scalar.copy(out=g_grouped[:, 0:taps, :, :].bitcast(F32), in_=by_word[:, 0:taps, :, :])
                 quantise_taps(SHIFTED, pair, g_grouped)
 
-        def shift_odd_channels():
-            odd_raw = g_raw[:, 0, G_ROW // 2 : G_ROW].rearrange("o (q e) -> o q e", e=2 * TAPS)
-            nc.scalar.copy(out=odd_left[:, :, TAPS - 1 : 2 * TAPS - 1], in_=odd_raw[:, :, TAPS : 2 * TAPS])
+        def shift_odd_channels(a):
+            odd_raw = g_raw[:, a, G_ROW // 2 : G_ROW].rearrange("o (q e) -> o q e", e=2 * TAPS)
+            nc.scalar.copy(out=odd_left[a][:, :, TAPS - 1 : 2 * TAPS - 1], in_=odd_raw[:, :, TAPS : 2 * TAPS])
 
         def empty_bank(pair, banks):
             taps = min(2, TAPS - 2 * pair)
@@ -236,7 +238,7 @@ def tile_model_pa_kernel(tc, x, grad_output, g, out):
             g2 = empty_bank(2, banks)
             x_grouped = new_stage()
             if between:
-                group_image(b, 0, x_grouped)
+                group_image(b, 0, x_grouped, nc.vector.tensor_copy)
                 group_extra(b)
             quantise_taps(a, 2, g2)
             g3 = empty_bank(3, banks)
@@ -244,9 +246,13 @@ def tile_model_pa_kernel(tc, x, grad_output, g, out):
             g4 = empty_bank(4, banks)
             quantise_taps(a, 4, g4)
             if not between:
-                group_image(b, 0, x_grouped)
+                group_image(b, 0, x_grouped, nc.vector.tensor_copy)
                 group_extra(b)
-            finish_band(b, x_grouped)
+            if a + 1 < SHIFTED:
+                shift_odd_channels(a + 1)
+                finish_band(b, x_grouped, nc.vector.tensor_copy)
+            else:
+                finish_band(b, x_grouped, nc.scalar.copy)
 
         def quantise_tile_in_pieces():
             for half in range(2):
@@ -299,11 +305,11 @@ def tile_model_pa_kernel(tc, x, grad_output, g, out):
 
         ctx.enter_context(tc.manual_schedule())
         x_grouped = new_stage()
-        group_image(0, 0, x_grouped)
+        group_image(0, 0, x_grouped, nc.vector.tensor_copy)
         group_extra(0)
-        finish_band(0, x_grouped)
+        finish_band(0, x_grouped, nc.scalar.copy)
         banks = new_banks()
-        shift_odd_channels()
+        shift_odd_channels(0)
         flip_channels(0, 0, banks)
         flip_channels(0, 1, banks)
         finish_tile_and_band(0, banks, 1, True)
@@ -329,9 +335,9 @@ def tile_model_pa_kernel(tc, x, grad_output, g, out):
                 finish_tile_and_band(1, banks, 2, False)
             if i == 1:
                 x_grouped = new_stage()
-                group_image(3, 0, x_grouped)
+                group_image(3, 0, x_grouped, nc.vector.tensor_copy)
                 group_extra(3)
-                finish_band(3, x_grouped)
+                finish_band(3, x_grouped, nc.scalar.copy)
                 order_tile()
             if (a, b) == (0, 3):
                 finish_ordered_tile(banks)

@@ -230,6 +230,48 @@ def tile_model_pa_kernel(tc, x, grad_output, g, out):
                 in_=g_grouped[:, 0:taps, :, :].rearrange("p k o t -> p (k o t)"),
             )
 
+        def empty_tap(tap, banks):
+            copy = nc.vector.tensor_copy if tap // 2 == 1 else nc.scalar.copy
+            g_one = g_stage.tile([P, P, PACK], BF16, align_bytes=64)
+            halves = banks[tap // 2][:].bitcast(BF16).rearrange("p t (o h) -> p h o t", h=2)
+            copy(out=g_one[:], in_=halves[:, tap % 2, :, :])
+            return g_one
+
+        def quantise_tap(a, tap, g_one):
+            nc.vector.quantize_mx(
+                out=g_codes[:, a, tap, :].bitcast(E5M2_X4),
+                scales=g_scales[:, a, tap, :],
+                in_=g_one[:].rearrange("p o t -> p (o t)"),
+            )
+
+        def finish_first_tile_and_band(banks):
+            x_grouped = new_stage()
+            t0 = empty_tap(0, banks)
+            t2 = empty_tap(2, banks)
+            quantise_tap(0, 0, t0)
+            t1 = empty_tap(1, banks)
+            quantise_tap(0, 1, t1)
+            t3 = empty_tap(3, banks)
+            t4 = empty_tap(4, banks)
+            quantise_tap(0, 2, t2)
+            quantise_tap(0, 3, t3)
+            t5 = empty_tap(5, banks)
+            quantise_tap(0, 4, t4)
+            group_image(1, 0, x_grouped, nc.vector.tensor_copy)
+            t6 = empty_tap(6, banks)
+            quantise_tap(0, 5, t5)
+            group_extra(1)
+            t7 = empty_tap(7, banks)
+            quantise_tap(0, 6, t6)
+            group_image(1, 1, x_grouped, nc.vector.tensor_copy)
+            t8 = empty_tap(8, banks)
+            quantise_tap(0, 7, t7)
+            quantise_tap(0, 8, t8)
+            shift_odd_channels(1)
+            quantise_x(1, x_grouped)
+            move_x(1, 1)
+            move_x(1, 2)
+
         def finish_tile_and_band(a, banks, b, between):
             g0 = empty_bank(0, banks)
             g1 = empty_bank(1, banks)
@@ -312,7 +354,7 @@ def tile_model_pa_kernel(tc, x, grad_output, g, out):
         shift_odd_channels(0)
         flip_channels(0, 0, banks)
         flip_channels(0, 1, banks)
-        finish_tile_and_band(0, banks, 1, True)
+        finish_first_tile_and_band(banks)
         by_kw = [kh * KW + kw for kw in range(KW) for kh in range(KH)]
         sequence = [(0, 0), (0, 1), (1, 0), (1, 1), (0, 2), (1, 2), (0, 3), (1, 3)]
         sequence += [(a, b) for a in range(SHIFTED, STEPS) for b in range(STEPS)]

@@ -28,10 +28,11 @@ QUANT_ROWS = 8
 G_ROW = CI * TAPS
 WORDS = PACK * TAPS // 2
 TAP_PAIRS = (TAPS + 1) // 2
+EARLY_MATMULS, LATE_MATMULS = 12, 4
 FLIPPED = 3
-SHIFTED = 2
 HALVES = PACK // 2
-RUN = 4
+CHUNKS = 4
+CHUNK_P = P // CHUNKS
 PIECE = PACK * TAPS
 PIECE_PITCH = 48
 HALF = P // 2
@@ -53,7 +54,7 @@ def tile_model_pa_kernel(tc, x, grad_output, g, out):
     nc = tc.nc
     with ExitStack() as ctx:
         keep = ctx.enter_context(tc.tile_pool(name="keep", bufs=1))
-        x_stage = ctx.enter_context(tc.tile_pool(name="x_stage", bufs=2 * KW))
+        x_stage = ctx.enter_context(tc.tile_pool(name="x_stage", bufs=3))
         g_stage = ctx.enter_context(tc.tile_pool(name="g_stage", bufs=TAP_PAIRS))
         piece_stage = ctx.enter_context(tc.tile_pool(name="piece_stage", bufs=KH))
         out_stage = ctx.enter_context(tc.tile_pool(name="out_stage", bufs=4))
@@ -63,9 +64,18 @@ def tile_model_pa_kernel(tc, x, grad_output, g, out):
         x_bands = [
             keep.tile([P, N_IMG, PACK, BAND, W], BF16, name="x_band%d" % s) for s in range(STEPS)
         ]
+
+        def x_rows(b, n):
+            first, end = band_rows(b)
+            return x_bands[b][:, n, :, 0 : end - first, :]
+
         g_raw = keep.tile([P, FLIPPED, G_ROW], BF16)
-        g_left = keep.tile([P, SHIFTED, G_ROW], BF16)
-        g_ordered = keep.tile([P, TAPS, HALVES, P, 2], BF16)
+        g_chunks = [keep.tile([P, G_ROW // CHUNKS], BF16, name="g_chunk%d" % h) for h in range(CHUNKS)]
+        g_left = keep.tile([P, G_ROW], BF16)
+        g_ordered = [
+            [keep.tile([P, KW, HALVES, P, 2], BF16, name="g_ordered%d_%d" % (a, kh)) for kh in range(KH)]
+            for a in range(FLIPPED)
+        ]
         g_pieces = keep.tile([P, P, PIECE_PITCH], BF16)
         identity = keep.tile([P, P], F32)
         x_codes = keep.tile([P, KW, H * ROW_COLS], U32, align_bytes=64)
@@ -76,15 +86,14 @@ def tile_model_pa_kernel(tc, x, grad_output, g, out):
         g_codes = keep.tile([P, STEPS, TAPS, P], U32, align_bytes=64)
         g_scales = keep.tile([P, STEPS, TAPS, P], U8, align_bytes=64)
 
+        idle_operand = keep.tile([P, N_COLS], BF16)
+        nc.vector.memset(idle_operand[:], 0.0)
+        scratch = keep.tile([P, 1], BF16)
+        nc.scalar.copy(out=scratch[:], in_=idle_operand[:, 0:1])
         make_identity(nc, identity[:])
         nc.vector.memset(x_extra[:], 0.0)
-        nc.vector.memset(g_left[:, :, G_ROW - 16 : G_ROW], 0.0)
-        odd_left = [
-            g_left[:, a, G_ROW // 2 : G_ROW].rearrange("o (q e) -> o q e", e=2 * TAPS) for a in range(SHIFTED)
-        ]
-        for a in range(SHIFTED):
-            nc.vector.memset(odd_left[a][:, :, 2 * TAPS - 2 : 2 * TAPS], 0.0)
-
+        odd_left = g_left[:, G_ROW // 2 :].rearrange("o (q e) -> o q e", e=2 * TAPS)
+        nc.vector.memset(odd_left[:, :, 2 * TAPS - 2 : 2 * TAPS], 0.0)
         g_rows = g.rearrange("o c kh kw -> o (c kh kw)")
         def load_band(s):
             first, end = band_rows(s)
@@ -95,14 +104,15 @@ def tile_model_pa_kernel(tc, x, grad_output, g, out):
                 )
 
         def load_tile(s):
-            o_rows = slice(s * P, (s + 1) * P)
-            nc.sync.dma_start(out=g_raw[:, s, :], in_=g_rows[o_rows, :])
-            if s < SHIFTED:
+            nc.sync.dma_start(out=g_raw[:, s, :], in_=g_rows[s * P : (s + 1) * P, :])
+            if s == 1:
                 left_end = G_ROW // 2
-                nc.sync.dma_start(out=g_left[:, s, 0:left_end], in_=g_rows[o_rows, 1 : left_end + 1])
+                nc.sync.dma_start(out=g_left[:, 0:left_end], in_=g_rows[P : 2 * P, 1 : left_end + 1])
 
+        for h in range(CHUNKS):
+            cols = slice(h * G_ROW // CHUNKS, (h + 1) * G_ROW // CHUNKS)
+            nc.sync.dma_start(out=g_chunks[h][:], in_=g_rows[0:P, cols])
         load_band(0)
-        load_tile(0)
         load_band(1)
         load_tile(1)
         load_band(2)
@@ -115,23 +125,24 @@ def tile_model_pa_kernel(tc, x, grad_output, g, out):
                 in_=g_rows[first_o : first_o + HALF, :].rearrange("o (p e) -> p o e", e=PIECE),
             )
 
-        def group_image(b, n, x_grouped, copy):
-            first, end = band_rows(b)
-            count = end - first
+        def group_rows(b, n, r0, r1, x_grouped, copy):
             copy(
-                out=x_grouped[:, 0:count, n, :, :].rearrange("p r (c i) t -> p r c t i", i=4),
-                in_=x_bands[b][:, n, :, 0:count, 0:WO].rearrange("p t r (c i) -> p r c t i", i=4),
+                out=x_grouped[:, r0:r1, n, :, :].rearrange("p r (c i) t -> p r c t i", i=4),
+                in_=x_rows(b, n)[:, :, r0:r1, 0:WO].rearrange("p t r (c i) -> p r c t i", i=4),
             )
 
-        def group_extra(b):
+        def group_image(b, n, x_grouped, copy):
+            first, end = band_rows(b)
+            group_rows(b, n, 0, end - first, x_grouped, copy)
+
+        def group_extra(b, copy):
             first, end = band_rows(b)
             count = end - first
-            nc.vector.tensor_copy(
-                out=x_extra[:, b, 0 : count * N_IMG * EXTRA, :].rearrange(
-                    "p (r n c) t -> p r n c t", n=N_IMG, c=EXTRA
-                ),
-                in_=x_bands[b][:, :, :, 0:count, WO:W].rearrange("p n t r c -> p r n c t"),
-            )
+            extra = x_extra[:, b, 0 : count * N_IMG * EXTRA, :].rearrange("p (r n c) t -> p r n c t", n=N_IMG, c=EXTRA)
+            for n in range(N_IMG):
+                copy(
+                    out=extra[:, :, n, :, :], in_=x_rows(b, n)[:, :, :, WO:W].rearrange("p t r c -> p r c t")
+                )
 
         def quantise_x(b, x_grouped):
             first, end = band_rows(b)
@@ -172,129 +183,64 @@ def tile_model_pa_kernel(tc, x, grad_output, g, out):
         def new_stage():
             return x_stage.tile([P, BAND, N_IMG, WO, PACK], BF16, align_bytes=64, name="x_grouped")
 
-        def finish_band(b, x_grouped, copy):
-            group_image(b, 1, x_grouped, copy)
-            quantise_x(b, x_grouped)
-            move_x(b, 1)
-            move_x(b, 2)
+        def order_channels(source, a, kh, p_range, copy):
+            by_tap = source.rearrange("o (p u e k) -> o u p e k", u=HALVES, e=2, k=TAPS)
+            copy(
+                out=g_ordered[a][kh][:, :, :, p_range, :].rearrange("o k u p e -> o u p e k"),
+                in_=by_tap[:, :, :, :, kh * KW : (kh + 1) * KW],
+            )
 
-        def flip_channels(a, parity, banks):
-            source = g_raw if parity == 0 else g_left
-            words = source[:, a, :].bitcast(F32).rearrange("o (p w) -> o w p", w=WORDS)
+        def order_tile(a, kh, copy):
+            order_channels(g_raw[:, a, :], a, kh, slice(0, P), copy)
+
+        def order_chunk(h, kh, copy):
+            order_channels(g_chunks[h][:], 0, kh, slice(h * CHUNK_P, (h + 1) * CHUNK_P), copy)
+
+        def flip_pair(a, pair, banks):
+            for tap in range(2 * pair, min(2 * pair + 2, TAPS)):
+                for u in range(HALVES):
+                    words = g_ordered[a][tap // KW][:, tap % KW, u, :, :].rearrange("o p e -> o (p e)").bitcast(F32)
+                    nc.tensor.transpose(banks[pair][:, (tap % 2) * HALVES + u, :], words, identity[:])
+
+        def shift_odd_channels():
+            odd_raw = g_raw[:, 1, G_ROW // 2 :].rearrange("o (q e) -> o q e", e=2 * TAPS)
+            nc.scalar.copy(out=odd_left[:, :, TAPS - 1 : 2 * TAPS - 1], in_=odd_raw[:, :, TAPS : 2 * TAPS])
+
+        def flip_channels(parity, banks):
+            source = g_raw[:, 1, :] if parity == 0 else g_left[:]
+            words = source.bitcast(F32).rearrange("o (p w) -> o w p", w=WORDS)
             for pair in range(TAP_PAIRS):
                 for t in range(parity, PACK, 2):
                     first_word = (t * TAPS) // 2
                     nc.tensor.transpose(banks[pair][:, t, :], words[:, first_word + pair, :], identity[:])
 
-        def order_tile():
-            by_tap = g_raw[:, SHIFTED, :].rearrange("o (p u e k) -> o u p e k", u=HALVES, e=2, k=TAPS)
-            for first_tap in range(0, TAPS, RUN):
-                taps = slice(first_tap, min(first_tap + RUN, TAPS))
-                nc.vector.tensor_copy(
-                    out=g_ordered[:, taps, :, :, :].rearrange("o k u p e -> o u p e k"),
-                    in_=by_tap[:, :, :, :, taps],
-                )
-
-        def flip_ordered_tile(banks):
-            for tap in range(TAPS):
-                for u in range(HALVES):
-                    words = g_ordered[:, tap, u, :, :].rearrange("o p e -> o (p e)").bitcast(F32)
-                    nc.tensor.transpose(banks[tap // 2][:, (tap % 2) * HALVES + u, :], words, identity[:])
-
-        def finish_ordered_tile(banks):
-            for pair in range(TAP_PAIRS):
-                taps = min(2, TAPS - 2 * pair)
-                g_grouped = g_stage.tile([P, 2, P, PACK], BF16, align_bytes=64)
-                by_word = banks[pair][:].rearrange("p (k u) o -> p k o u", u=HALVES)
-                nc.scalar.copy(out=g_grouped[:, 0:taps, :, :].bitcast(F32), in_=by_word[:, 0:taps, :, :])
-                quantise_taps(SHIFTED, pair, g_grouped)
-
-        def shift_odd_channels(a):
-            odd_raw = g_raw[:, a, G_ROW // 2 : G_ROW].rearrange("o (q e) -> o q e", e=2 * TAPS)
-            nc.scalar.copy(out=odd_left[a][:, :, TAPS - 1 : 2 * TAPS - 1], in_=odd_raw[:, :, TAPS : 2 * TAPS])
-
-        def empty_bank(pair, banks):
+        def empty_bank(pair, banks, copy):
             taps = min(2, TAPS - 2 * pair)
-            copy = nc.vector.tensor_copy if pair == 1 else nc.scalar.copy
             g_grouped = g_stage.tile([P, 2, P, PACK], BF16, align_bytes=64)
             halves = banks[pair][:].bitcast(BF16).rearrange("p t (o h) -> p h o t", h=2)
             copy(out=g_grouped[:, 0:taps, :, :], in_=halves[:, 0:taps, :, :])
             return g_grouped
 
-        def quantise_taps(a, pair, g_grouped):
-            taps = min(2, TAPS - 2 * pair)
-            tap_range = slice(2 * pair, 2 * pair + taps)
+        def flip_tile(a, banks):
+            for pair in range(TAP_PAIRS):
+                flip_pair(a, pair, banks)
+
+        def empty_taps(taps, banks, copy):
+            count = taps.stop - taps.start
+            pair = taps.start // 2
+            g_grouped = g_stage.tile([P, 2, P, PACK], BF16, align_bytes=64)
+            by_word = banks[pair][:].rearrange("p (k u) o -> p k o u", u=HALVES)
+            in_bank = slice(taps.start - 2 * pair, taps.stop - 2 * pair)
+            copy(out=g_grouped[:, 0:count, :, :].bitcast(F32), in_=by_word[:, in_bank, :, :])
+            return g_grouped
+
+        def quantise_taps(a, taps, g_grouped):
+            count = taps.stop - taps.start
             nc.vector.quantize_mx(
-                out=g_codes[:, a, tap_range, :].rearrange("p k o -> p (k o)").bitcast(E5M2_X4),
-                scales=g_scales[:, a, tap_range, :].rearrange("p k o -> p (k o)"),
-                in_=g_grouped[:, 0:taps, :, :].rearrange("p k o t -> p (k o t)"),
+                out=g_codes[:, a, taps, :].rearrange("p k o -> p (k o)").bitcast(E5M2_X4),
+                scales=g_scales[:, a, taps, :].rearrange("p k o -> p (k o)"),
+                in_=g_grouped[:, 0:count, :, :].rearrange("p k o t -> p (k o t)"),
             )
-
-        def empty_tap(tap, banks):
-            copy = nc.vector.tensor_copy if tap // 2 == 1 else nc.scalar.copy
-            g_one = g_stage.tile([P, P, PACK], BF16, align_bytes=64)
-            halves = banks[tap // 2][:].bitcast(BF16).rearrange("p t (o h) -> p h o t", h=2)
-            copy(out=g_one[:], in_=halves[:, tap % 2, :, :])
-            return g_one
-
-        def quantise_tap(a, tap, g_one):
-            nc.vector.quantize_mx(
-                out=g_codes[:, a, tap, :].bitcast(E5M2_X4),
-                scales=g_scales[:, a, tap, :],
-                in_=g_one[:].rearrange("p o t -> p (o t)"),
-            )
-
-        def finish_first_tile_and_band(banks):
-            x_grouped = new_stage()
-            t0 = empty_tap(0, banks)
-            t2 = empty_tap(2, banks)
-            quantise_tap(0, 0, t0)
-            t1 = empty_tap(1, banks)
-            quantise_tap(0, 1, t1)
-            t3 = empty_tap(3, banks)
-            t4 = empty_tap(4, banks)
-            quantise_tap(0, 2, t2)
-            quantise_tap(0, 3, t3)
-            t5 = empty_tap(5, banks)
-            quantise_tap(0, 4, t4)
-            group_image(1, 0, x_grouped, nc.vector.tensor_copy)
-            t6 = empty_tap(6, banks)
-            quantise_tap(0, 5, t5)
-            group_extra(1)
-            t7 = empty_tap(7, banks)
-            quantise_tap(0, 6, t6)
-            group_image(1, 1, x_grouped, nc.vector.tensor_copy)
-            t8 = empty_tap(8, banks)
-            quantise_tap(0, 7, t7)
-            quantise_tap(0, 8, t8)
-            shift_odd_channels(1)
-            quantise_x(1, x_grouped)
-            move_x(1, 1)
-            move_x(1, 2)
-
-        def finish_tile_and_band(a, banks, b, between):
-            g0 = empty_bank(0, banks)
-            g1 = empty_bank(1, banks)
-            quantise_taps(a, 0, g0)
-            quantise_taps(a, 1, g1)
-            g2 = empty_bank(2, banks)
-            x_grouped = new_stage()
-            if between:
-                group_image(b, 0, x_grouped, nc.vector.tensor_copy)
-                group_extra(b)
-            quantise_taps(a, 2, g2)
-            g3 = empty_bank(3, banks)
-            quantise_taps(a, 3, g3)
-            g4 = empty_bank(4, banks)
-            quantise_taps(a, 4, g4)
-            if not between:
-                group_image(b, 0, x_grouped, nc.vector.tensor_copy)
-                group_extra(b)
-            if a + 1 < SHIFTED:
-                shift_odd_channels(a + 1)
-                finish_band(b, x_grouped, nc.vector.tensor_copy)
-            else:
-                finish_band(b, x_grouped, nc.scalar.copy)
 
         def quantise_tile_in_pieces():
             for half in range(2):
@@ -330,6 +276,11 @@ def tile_model_pa_kernel(tc, x, grad_output, g, out):
                 stop=stop,
             )
 
+        def idle_matmuls(count):
+            sums = sum_banks.tile([P, N_COLS], F32)
+            for unused in range(count):
+                nc.tensor.matmul(sums[:], lhsT=idle_operand[:, 0:P], rhs=idle_operand[:], start=True, stop=True)
+
         def store_product(a, b, sums):
             skip = b * ROWS - first_output_row(b)
             fresh = ROWS - skip
@@ -346,41 +297,90 @@ def tile_model_pa_kernel(tc, x, grad_output, g, out):
             )
 
         ctx.enter_context(tc.manual_schedule())
-        x_grouped = new_stage()
-        group_image(0, 0, x_grouped, nc.vector.tensor_copy)
-        group_extra(0)
-        finish_band(0, x_grouped, nc.scalar.copy)
+        by_vector, by_scalar = nc.vector.tensor_copy, nc.scalar.copy
+
+        def pair_taps(pair):
+            return slice(2 * pair, min(2 * pair + 2, TAPS))
+
+        for h in range(CHUNKS):
+            order_chunk(h, 0, by_vector)
+            order_chunk(h, 2, by_scalar)
+            order_chunk(h, 1, by_vector)
+        idle_matmuls(EARLY_MATMULS)
         banks = new_banks()
-        shift_odd_channels(0)
-        flip_channels(0, 0, banks)
-        flip_channels(0, 1, banks)
-        finish_first_tile_and_band(banks)
+        flip_tile(0, banks)
+        idle_matmuls(LATE_MATMULS)
+
+        x_grouped = new_stage()
+        group_rows(0, 0, 0, BAND, x_grouped, by_vector)
+        pair_0 = empty_taps(pair_taps(0), banks, by_scalar)
+        group_rows(0, 1, 4, BAND, x_grouped, by_scalar)
+        group_rows(0, 1, 0, 4, x_grouped, by_vector)
+        group_extra(0, by_scalar)
+        quantise_taps(0, pair_taps(0), pair_0)
+        pair_1 = empty_taps(pair_taps(1), banks, by_scalar)
+        quantise_x(0, x_grouped)
+        pair_3 = empty_taps(pair_taps(3), banks, by_scalar)
+        quantise_taps(0, pair_taps(1), pair_1)
+        move_x(0, 1)
+        pair_2 = empty_taps(pair_taps(2), banks, by_scalar)
+        quantise_taps(0, pair_taps(3), pair_3)
+        pair_4 = empty_taps(pair_taps(4), banks, by_scalar)
+        quantise_taps(0, pair_taps(2), pair_2)
+        move_x(0, 2)
+        quantise_taps(0, pair_taps(4), pair_4)
+
+        x_grouped = new_stage()
+        group_image(1, 0, x_grouped, by_scalar)
+        group_image(1, 1, x_grouped, by_scalar)
+        group_extra(1, by_vector)
+        shift_odd_channels()
+        quantise_x(1, x_grouped)
+        move_x(1, 1)
+        move_x(1, 2)
+
         by_kw = [kh * KW + kw for kw in range(KW) for kh in range(KH)]
+        first_order = [0, 3, 6, 1, 7, 4, 2, 5, 8]
         sequence = [(0, 0), (0, 1), (1, 0), (1, 1), (0, 2), (1, 2), (0, 3), (1, 3)]
-        sequence += [(a, b) for a in range(SHIFTED, STEPS) for b in range(STEPS)]
+        sequence += [(a, b) for a in range(2, STEPS) for b in range(STEPS)]
         for i, (a, b) in enumerate(sequence):
-            if i == 0:
-                banks = new_banks()
             sums = sum_banks.tile([P, N_COLS], F32)
-            order = by_kw if (a == 0 and b > 0) else list(range(TAPS))
+            order = first_order if i == 0 else by_kw if a == 0 else list(range(TAPS))
+            if i == 1:
+                banks = new_banks()
+                flip_channels(0, banks)
             for j, tap in enumerate(order):
                 one_pass(a, b, tap, sums, j == 0, j == TAPS - 1)
-                if i == 0 and j == 3:
-                    flip_channels(1, 0, banks)
-            if i == 0:
-                flip_channels(1, 1, banks)
-            if (a, b) == (0, 3):
-                banks = new_banks()
-                flip_ordered_tile(banks)
-            store_product(a, b, sums)
-            if i == 0:
-                finish_tile_and_band(1, banks, 2, False)
+                if i == 1 and j == 1:
+                    flip_channels(1, banks)
+                if (a, b) == (0, 3) and j == 8:
+                    banks = new_banks()
+                    flip_tile(2, banks)
             if i == 1:
+                g0 = empty_bank(0, banks, by_scalar)
+                g1 = empty_bank(1, banks, by_vector)
+                quantise_taps(1, pair_taps(0), g0)
+                g2 = empty_bank(2, banks, by_scalar)
+                quantise_taps(1, pair_taps(1), g1)
+                g3 = empty_bank(3, banks, by_vector)
+                quantise_taps(1, pair_taps(2), g2)
+                g4 = empty_bank(4, banks, by_scalar)
+                quantise_taps(1, pair_taps(3), g3)
+                quantise_taps(1, pair_taps(4), g4)
+            store_product(a, b, sums)
+            if i in (1, 2):
                 x_grouped = new_stage()
-                group_image(3, 0, x_grouped, nc.vector.tensor_copy)
-                group_extra(3)
-                finish_band(3, x_grouped, nc.scalar.copy)
-                order_tile()
+                group_image(i + 1, 0, x_grouped, by_vector)
+                group_image(i + 1, 1, x_grouped, by_scalar)
+                group_extra(i + 1, by_vector)
+                quantise_x(i + 1, x_grouped)
+                move_x(i + 1, 1)
+                move_x(i + 1, 2)
+            if i == 2:
+                for kh in range(KH):
+                    order_tile(2, kh, by_vector)
             if (a, b) == (0, 3):
-                finish_ordered_tile(banks)
+                for pair in range(TAP_PAIRS):
+                    g_grouped = empty_taps(pair_taps(pair), banks, by_scalar)
+                    quantise_taps(2, pair_taps(pair), g_grouped)
                 quantise_tile_in_pieces()

@@ -22,6 +22,9 @@ ROWS = 8
 ROW_COLS = N_IMG * WO
 N_COLS = ROWS * ROW_COLS
 BAND = ROWS + KH - 1
+LAST_ROW = HO // ROWS * ROWS
+BLOCK_ROWS = P // ROW_COLS
+BLOCKS = (HO - LAST_ROW) // BLOCK_ROWS
 EXTRA = W - WO
 EXTRA_PIXELS = 64
 QUANT_ROWS = 8
@@ -42,12 +45,12 @@ BYTES = 2 * N_IMG * CI * H * W + 2 * CO * CI * TAPS + 4 * N_IMG * CO * HO * WO
 
 
 def first_output_row(b):
-    return min(b * ROWS, HO - ROWS)
+    return b * ROWS
 
 
 def band_rows(b):
     first = 0 if b == 0 else first_output_row(b - 1) + BAND
-    return first, first_output_row(b) + BAND
+    return first, min(first_output_row(b) + BAND, H)
 
 
 def tile_model_pa_kernel(tc, x, grad_output, g, out):
@@ -58,6 +61,7 @@ def tile_model_pa_kernel(tc, x, grad_output, g, out):
         g_stage = ctx.enter_context(tc.tile_pool(name="g_stage", bufs=TAP_PAIRS))
         piece_stage = ctx.enter_context(tc.tile_pool(name="piece_stage", bufs=KH))
         out_stage = ctx.enter_context(tc.tile_pool(name="out_stage", bufs=4))
+        block_stage = ctx.enter_context(tc.tile_pool(name="block_stage", bufs=BLOCKS))
         flip_banks = ctx.enter_context(tc.psum_pool(name="flip_banks", bufs=TAP_PAIRS))
         sum_banks = ctx.enter_context(tc.psum_pool(name="sum_banks", bufs=8 - TAP_PAIRS))
 
@@ -83,8 +87,8 @@ def tile_model_pa_kernel(tc, x, grad_output, g, out):
         x_extra = keep.tile([P, STEPS, EXTRA_PIXELS, PACK], BF16, align_bytes=64)
         extra_codes = keep.tile([P, STEPS, EXTRA_PIXELS], U32, align_bytes=64)
         extra_scales = keep.tile([P, STEPS, EXTRA_PIXELS], U8, align_bytes=64)
-        g_codes = keep.tile([P, STEPS, TAPS, P], U32, align_bytes=64)
-        g_scales = keep.tile([P, STEPS, TAPS, P], U8, align_bytes=64)
+        g_codes = keep.tile([P, TAPS, STEPS, P], U32, align_bytes=64)
+        g_scales = keep.tile([P, TAPS, STEPS, P], U8, align_bytes=64)
 
         idle_operand = keep.tile([P, N_COLS], BF16)
         nc.vector.memset(idle_operand[:], 0.0)
@@ -92,7 +96,7 @@ def tile_model_pa_kernel(tc, x, grad_output, g, out):
         nc.scalar.copy(out=scratch[:], in_=idle_operand[:, 0:1])
         make_identity(nc, identity[:])
         nc.vector.memset(x_extra[:], 0.0)
-        odd_left = g_left[:, G_ROW // 2 :].rearrange("o (q e) -> o q e", e=2 * TAPS)
+        odd_left = g_left[:].rearrange("o (q e) -> o q e", e=2 * TAPS)
         nc.vector.memset(odd_left[:, :, 2 * TAPS - 2 : 2 * TAPS], 0.0)
         g_rows = g.rearrange("o c kh kw -> o (c kh kw)")
         def load_band(s):
@@ -105,9 +109,6 @@ def tile_model_pa_kernel(tc, x, grad_output, g, out):
 
         def load_tile(s):
             nc.sync.dma_start(out=g_raw[:, s, :], in_=g_rows[s * P : (s + 1) * P, :])
-            if s == 1:
-                left_end = G_ROW // 2
-                nc.sync.dma_start(out=g_left[:, 0:left_end], in_=g_rows[P : 2 * P, 1 : left_end + 1])
 
         for h in range(CHUNKS):
             cols = slice(h * G_ROW // CHUNKS, (h + 1) * G_ROW // CHUNKS)
@@ -116,7 +117,6 @@ def tile_model_pa_kernel(tc, x, grad_output, g, out):
         load_band(1)
         load_tile(1)
         load_band(2)
-        load_band(3)
         load_tile(2)
         for half in range(2):
             first_o = FLIPPED * P + half * HALF
@@ -124,6 +124,8 @@ def tile_model_pa_kernel(tc, x, grad_output, g, out):
                 out=g_pieces[:, half * HALF : (half + 1) * HALF, 0:PIECE],
                 in_=g_rows[first_o : first_o + HALF, :].rearrange("o (p e) -> p o e", e=PIECE),
             )
+            if half == 0:
+                load_band(3)
 
         def group_rows(b, n, r0, r1, x_grouped, copy):
             copy(
@@ -203,7 +205,7 @@ def tile_model_pa_kernel(tc, x, grad_output, g, out):
                     nc.tensor.transpose(banks[pair][:, (tap % 2) * HALVES + u, :], words, identity[:])
 
         def shift_odd_channels():
-            odd_raw = g_raw[:, 1, G_ROW // 2 :].rearrange("o (q e) -> o q e", e=2 * TAPS)
+            odd_raw = g_raw[:, 1, :].rearrange("o (q e) -> o q e", e=2 * TAPS)
             nc.scalar.copy(out=odd_left[:, :, TAPS - 1 : 2 * TAPS - 1], in_=odd_raw[:, :, TAPS : 2 * TAPS])
 
         def flip_channels(parity, banks):
@@ -235,12 +237,12 @@ def tile_model_pa_kernel(tc, x, grad_output, g, out):
             return g_grouped
 
         def quantise_taps(a, taps, g_grouped):
-            count = taps.stop - taps.start
-            nc.vector.quantize_mx(
-                out=g_codes[:, a, taps, :].rearrange("p k o -> p (k o)").bitcast(E5M2_X4),
-                scales=g_scales[:, a, taps, :].rearrange("p k o -> p (k o)"),
-                in_=g_grouped[:, 0:count, :, :].rearrange("p k o t -> p (k o t)"),
-            )
+            for k, tap in enumerate(range(taps.start, taps.stop)):
+                nc.vector.quantize_mx(
+                    out=g_codes[:, tap, a, :].bitcast(E5M2_X4),
+                    scales=g_scales[:, tap, a, :],
+                    in_=g_grouped[:, k, :, :].rearrange("p o t -> p (o t)"),
+                )
 
         def quantise_tile_in_pieces():
             for half in range(2):
@@ -254,8 +256,8 @@ def tile_model_pa_kernel(tc, x, grad_output, g, out):
                     )
                     for kw in range(KW):
                         nc.vector.quantize_mx(
-                            out=g_codes[:, FLIPPED, kh * KW + kw, o_half].bitcast(E5M2_X4),
-                            scales=g_scales[:, FLIPPED, kh * KW + kw, o_half],
+                            out=g_codes[:, kh * KW + kw, FLIPPED, o_half].bitcast(E5M2_X4),
+                            scales=g_scales[:, kh * KW + kw, FLIPPED, o_half],
                             in_=piece_grouped[:, kw, :, :].rearrange("p o t -> p (o t)"),
                         )
 
@@ -268,10 +270,24 @@ def tile_model_pa_kernel(tc, x, grad_output, g, out):
             cols = slice(first_col, first_col + N_COLS)
             nc.tensor.matmul_mx(
                 out=sums[:],
-                lhsT=g_codes[:, a, tap, :].bitcast(E5M2_X4),
-                lhsT_scale=g_scales[:, a, tap, :],
+                lhsT=g_codes[:, tap, a, :].bitcast(E5M2_X4),
+                lhsT_scale=g_scales[:, tap, a, :],
                 rhs=x_codes[:, kw, cols].bitcast(E4M3_X4),
                 rhs_scale=x_scales[:, kw, cols],
+                start=start,
+                stop=stop,
+            )
+
+        def block_pass(k, tap, sums, start, stop):
+            kh, kw = divmod(tap, KW)
+            first_col = (LAST_ROW + k * BLOCK_ROWS + kh) * ROW_COLS
+            cols = slice(first_col, first_col + P)
+            nc.tensor.matmul_mx(
+                out=sums[:],
+                lhsT=x_codes[:, kw, cols].bitcast(E4M3_X4),
+                lhsT_scale=x_scales[:, kw, cols],
+                rhs=g_codes[:, tap, :, :].rearrange("p a o -> p (a o)").bitcast(E5M2_X4),
+                rhs_scale=g_scales[:, tap, :, :].rearrange("p a o -> p (a o)"),
                 start=start,
                 stop=stop,
             )
@@ -282,18 +298,11 @@ def tile_model_pa_kernel(tc, x, grad_output, g, out):
                 nc.tensor.matmul(sums[:], lhsT=idle_operand[:, 0:P], rhs=idle_operand[:], start=True, stop=True)
 
         def store_product(a, b, sums):
-            skip = b * ROWS - first_output_row(b)
-            fresh = ROWS - skip
             result = out_stage.tile([P, N_IMG, ROWS, WO], F32)
-            nc.scalar.copy(
-                out=result[:, :, 0:fresh, :],
-                in_=sums[:].rearrange("p (i n j) -> p n i j", n=N_IMG, j=WO)[:, :, skip:ROWS, :],
-            )
+            nc.scalar.copy(out=result[:], in_=sums[:].rearrange("p (i n j) -> p n i j", n=N_IMG, j=WO))
             nc.scalar.dma_start(
-                out=out[:, a * P : (a + 1) * P, b * ROWS : b * ROWS + fresh, :].rearrange(
-                    "n o i j -> o n (i j)"
-                ),
-                in_=result[:, :, 0:fresh, :].rearrange("p n i j -> p n (i j)"),
+                out=out[:, a * P : (a + 1) * P, b * ROWS : (b + 1) * ROWS, :].rearrange("n o i j -> o n (i j)"),
+                in_=result[:].rearrange("p n i j -> p n (i j)"),
             )
 
         ctx.enter_context(tc.manual_schedule())
@@ -331,7 +340,7 @@ def tile_model_pa_kernel(tc, x, grad_output, g, out):
         quantise_taps(0, pair_taps(4), pair_4)
 
         x_grouped = new_stage()
-        group_image(1, 0, x_grouped, by_scalar)
+        group_image(1, 0, x_grouped, by_vector)
         group_image(1, 1, x_grouped, by_scalar)
         group_extra(1, by_vector)
         shift_odd_channels()
@@ -341,21 +350,29 @@ def tile_model_pa_kernel(tc, x, grad_output, g, out):
 
         by_kw = [kh * KW + kw for kw in range(KW) for kh in range(KH)]
         first_order = [0, 3, 6, 1, 7, 4, 2, 5, 8]
-        sequence = [(0, 0), (0, 1), (1, 0), (1, 1), (0, 2), (1, 2), (0, 3), (1, 3)]
-        sequence += [(a, b) for a in range(2, STEPS) for b in range(STEPS)]
+        def prepare_band(b):
+            x_grouped = new_stage()
+            group_image(b, 0, x_grouped, by_vector)
+            group_image(b, 1, x_grouped, by_scalar)
+            group_extra(b, by_vector)
+            quantise_x(b, x_grouped)
+            move_x(b, 1)
+            move_x(b, 2)
+
+        sequence = [(0, 0), (0, 1), (1, 0), (1, 1), (0, 2), (1, 2), (2, 0), (2, 1), (2, 2)]
         for i, (a, b) in enumerate(sequence):
             sums = sum_banks.tile([P, N_COLS], F32)
             order = first_order if i == 0 else by_kw if a == 0 else list(range(TAPS))
-            if i == 1:
-                banks = new_banks()
-                flip_channels(0, banks)
             for j, tap in enumerate(order):
                 one_pass(a, b, tap, sums, j == 0, j == TAPS - 1)
+                if i == 0 and j == 1:
+                    banks = new_banks()
+                    flip_channels(0, banks)
                 if i == 1 and j == 1:
                     flip_channels(1, banks)
-                if (a, b) == (0, 3) and j == 8:
-                    banks = new_banks()
-                    flip_tile(2, banks)
+            if (a, b) == (0, 2):
+                banks = new_banks()
+                flip_tile(2, banks)
             if i == 1:
                 g0 = empty_bank(0, banks, by_scalar)
                 g1 = empty_bank(1, banks, by_vector)
@@ -368,19 +385,45 @@ def tile_model_pa_kernel(tc, x, grad_output, g, out):
                 quantise_taps(1, pair_taps(3), g3)
                 quantise_taps(1, pair_taps(4), g4)
             store_product(a, b, sums)
-            if i in (1, 2):
-                x_grouped = new_stage()
-                group_image(i + 1, 0, x_grouped, by_vector)
-                group_image(i + 1, 1, x_grouped, by_scalar)
-                group_extra(i + 1, by_vector)
-                quantise_x(i + 1, x_grouped)
-                move_x(i + 1, 1)
-                move_x(i + 1, 2)
-            if i == 2:
+            if i == 1:
+                prepare_band(2)
                 for kh in range(KH):
                     order_tile(2, kh, by_vector)
-            if (a, b) == (0, 3):
+            if (a, b) == (0, 2):
                 for pair in range(TAP_PAIRS):
                     g_grouped = empty_taps(pair_taps(pair), banks, by_scalar)
                     quantise_taps(2, pair_taps(pair), g_grouped)
+                prepare_band(3)
                 quantise_tile_in_pieces()
+
+        block_sums = []
+        for k in range(BLOCKS):
+            sums = sum_banks.tile([P, N_COLS], F32)
+            for tap in range(TAPS):
+                block_pass(k, tap, sums, tap == 0, tap == TAPS - 1)
+            pixels = block_stage.tile([P, CO], F32)
+            nc.scalar.copy(out=pixels[:], in_=sums[:])
+            block_sums.append(pixels)
+        last_rows = keep.tile([P, STEPS, N_IMG, BLOCKS * BLOCK_ROWS, WO], F32)
+        for b in range(STEPS - 1):
+            sums = sum_banks.tile([P, N_COLS], F32)
+            for tap in range(TAPS):
+                one_pass(STEPS - 1, b, tap, sums, tap == 0, tap == TAPS - 1)
+            if b == 0:
+                banks = [flip_banks.tile([P, STEPS, P], F32, name="flipped") for k in range(BLOCKS)]
+                for k in range(BLOCKS):
+                    for a in range(STEPS):
+                        nc.tensor.transpose(banks[k][:, a, :], block_sums[k][:, a * P : (a + 1) * P], identity[:])
+            store_product(STEPS - 1, b, sums)
+            if b == 0:
+                for k in range(BLOCKS):
+                    rows = slice(k * BLOCK_ROWS, (k + 1) * BLOCK_ROWS)
+                    nc.scalar.copy(
+                        out=last_rows[:, :, :, rows, :],
+                        in_=banks[k][:].rearrange("p a (r n j) -> p a n r j", n=N_IMG, j=WO),
+                    )
+                for a in range(STEPS):
+                    nc.scalar.dma_start(
+                        out=out[:, a * P : (a + 1) * P, LAST_ROW:HO, :].rearrange("n o i j -> o n (i j)"),
+                        in_=last_rows[:, a, :, :, :].rearrange("p n r j -> p n (r j)"),
+                    )

@@ -32,6 +32,7 @@ G_ROW = CI * TAPS
 WORDS = PACK * TAPS // 2
 TAP_PAIRS = (TAPS + 1) // 2
 EARLY_MATMULS, LATE_MATMULS = 12, 4
+PENDING = 10
 FLIPPED = 3
 HALVES = PACK // 2
 CHUNKS = 4
@@ -60,7 +61,7 @@ def tile_model_pa_kernel(tc, x, grad_output, g, out):
         x_stage = ctx.enter_context(tc.tile_pool(name="x_stage", bufs=3))
         g_stage = ctx.enter_context(tc.tile_pool(name="g_stage", bufs=TAP_PAIRS))
         piece_stage = ctx.enter_context(tc.tile_pool(name="piece_stage", bufs=KH))
-        out_stage = ctx.enter_context(tc.tile_pool(name="out_stage", bufs=4))
+        out_stage = ctx.enter_context(tc.tile_pool(name="out_stage", bufs=PENDING))
         block_stage = ctx.enter_context(tc.tile_pool(name="block_stage", bufs=BLOCKS))
         flip_banks = ctx.enter_context(tc.psum_pool(name="flip_banks", bufs=TAP_PAIRS))
         sum_banks = ctx.enter_context(tc.psum_pool(name="sum_banks", bufs=8 - TAP_PAIRS))
@@ -300,7 +301,8 @@ def tile_model_pa_kernel(tc, x, grad_output, g, out):
         def store_product(a, b, sums):
             result = out_stage.tile([P, N_IMG, ROWS, WO], F32)
             nc.scalar.copy(out=result[:], in_=sums[:].rearrange("p (i n j) -> p n i j", n=N_IMG, j=WO))
-            nc.scalar.dma_start(
+            queue = nc.sync if a < STEPS - 1 else nc.scalar
+            queue.dma_start(
                 out=out[:, a * P : (a + 1) * P, b * ROWS : (b + 1) * ROWS, :].rearrange("n o i j -> o n (i j)"),
                 in_=result[:].rearrange("p n i j -> p n (i j)"),
             )

@@ -54,6 +54,9 @@ def band_rows(b):
     return first, min(first_output_row(b) + BAND, H)
 
 
+LOADED_ROWS = (band_rows(0), band_rows(1), (band_rows(2)[0], H))
+
+
 def tile_model_pa_kernel(tc, x, grad_output, g, out):
     nc = tc.nc
     with ExitStack() as ctx:
@@ -67,12 +70,15 @@ def tile_model_pa_kernel(tc, x, grad_output, g, out):
         sum_banks = ctx.enter_context(tc.psum_pool(name="sum_banks", bufs=8 - TAP_PAIRS))
 
         x_bands = [
-            keep.tile([P, N_IMG, PACK, BAND, W], BF16, name="x_band%d" % s) for s in range(STEPS)
+            keep.tile([P, N_IMG, PACK, end - first, W], BF16, name="x_band%d" % k)
+            for k, (first, end) in enumerate(LOADED_ROWS)
         ]
 
         def x_rows(b, n):
             first, end = band_rows(b)
-            return x_bands[b][:, n, :, 0 : end - first, :]
+            k = min(b, len(LOADED_ROWS) - 1)
+            start = LOADED_ROWS[k][0]
+            return x_bands[k][:, n, :, first - start : end - start, :]
 
         g_raw = keep.tile([P, FLIPPED, G_ROW], BF16)
         g_chunks = [keep.tile([P, G_ROW // CHUNKS], BF16, name="g_chunk%d" % h) for h in range(CHUNKS)]
@@ -101,10 +107,10 @@ def tile_model_pa_kernel(tc, x, grad_output, g, out):
         nc.vector.memset(odd_left[:, :, 2 * TAPS - 2 : 2 * TAPS], 0.0)
         g_rows = g.rearrange("o c kh kw -> o (c kh kw)")
         def load_band(s):
-            first, end = band_rows(s)
+            first, end = LOADED_ROWS[s]
             for n in range(N_IMG):
                 nc.sync.dma_start(
-                    out=x_bands[s][:, n, :, 0 : end - first, :].rearrange("p t r c -> p t (r c)"),
+                    out=x_bands[s][:, n, :, :, :].rearrange("p t r c -> p t (r c)"),
                     in_=x[n, :, first:end, :].rearrange("(p t) r c -> p t (r c)", t=PACK),
                 )
 
@@ -125,8 +131,6 @@ def tile_model_pa_kernel(tc, x, grad_output, g, out):
                 out=g_pieces[:, half * HALF : (half + 1) * HALF, 0:PIECE],
                 in_=g_rows[first_o : first_o + HALF, :].rearrange("o (p e) -> p o e", e=PIECE),
             )
-            if half == 0:
-                load_band(3)
 
         def group_rows(b, n, r0, r1, x_grouped, copy):
             copy(
@@ -398,13 +402,14 @@ def tile_model_pa_kernel(tc, x, grad_output, g, out):
                 prepare_band(3)
                 quantise_tile_in_pieces()
 
+        sums = [flip_banks.tile([P, N_COLS], F32, name="flipped") for k in range(BLOCKS)]
+        for tap in range(TAPS):
+            for k in range(BLOCKS):
+                block_pass(k, tap, sums[k], tap == 0, tap == TAPS - 1)
         block_sums = []
         for k in range(BLOCKS):
-            sums = sum_banks.tile([P, N_COLS], F32)
-            for tap in range(TAPS):
-                block_pass(k, tap, sums, tap == 0, tap == TAPS - 1)
             pixels = block_stage.tile([P, CO], F32)
-            nc.scalar.copy(out=pixels[:], in_=sums[:])
+            nc.scalar.copy(out=pixels[:], in_=sums[k][:])
             block_sums.append(pixels)
         last_rows = keep.tile([P, STEPS, N_IMG, BLOCKS * BLOCK_ROWS, WO], F32)
         for b in range(STEPS - 1):

from contextlib import ExitStack

import concourse.mybir as mybir
from concourse.masks import make_identity

BF16 = mybir.dt.bfloat16
F32 = mybir.dt.float32
U32 = mybir.dt.uint32
U8 = mybir.dt.uint8
I32 = mybir.dt.int32
E4M3_X4 = mybir.dt.float8_e4m3fn_x4
E5M2_X4 = mybir.dt.float8_e5m2_x4

N_IMG, CI, CO, H, W, KH, KW = 2, 512, 512, 32, 34, 3, 3
HO, WO = H - KH + 1, W - KW + 1
TAPS = KH * KW

P = 128
PACK = 4
STEPS = CO // P
ROWS = 8
ROW_COLS = N_IMG * WO
N_COLS = ROWS * ROW_COLS
BAND = ROWS + KH - 1
LAST_ROW = HO // ROWS * ROWS
BLOCK_ROWS = P // ROW_COLS
BLOCKS = (HO - LAST_ROW) // BLOCK_ROWS
EXTRA = W - WO
EXTRA_PIXELS = 64
QUANT_ROWS = 8
G_ROW = CI * TAPS
WORDS = PACK * TAPS // 2
TAP_PAIRS = (TAPS + 1) // 2
EARLY_MATMULS, LATE_MATMULS = 12, 4
PENDING = 10
FLIPPED = 3
HALVES = PACK // 2
CHUNKS = 4
CHUNK_P = P // CHUNKS
PIECE = PACK * TAPS
PIECE_PITCH = 48
HALF = P // 2

FLOPS = 2 * CO * CI * TAPS * N_IMG * HO * WO
BYTES = 2 * N_IMG * CI * H * W + 2 * CO * CI * TAPS + 4 * N_IMG * CO * HO * WO


def first_output_row(b):
    return b * ROWS


def band_rows(b):
    first = 0 if b == 0 else first_output_row(b - 1) + BAND
    return first, min(first_output_row(b) + BAND, H)


LOADED_ROWS = (band_rows(0), band_rows(1), (band_rows(2)[0], H))


def tile_model_pa_kernel(tc, x, grad_output, g, out):
    nc = tc.nc
    with ExitStack() as ctx:
        keep = ctx.enter_context(tc.tile_pool(name="keep", bufs=1))
        x_stage = ctx.enter_context(tc.tile_pool(name="x_stage", bufs=3))
        g_stage = ctx.enter_context(tc.tile_pool(name="g_stage", bufs=TAP_PAIRS))
        piece_stage = ctx.enter_context(tc.tile_pool(name="piece_stage", bufs=KH))
        out_stage = ctx.enter_context(tc.tile_pool(name="out_stage", bufs=PENDING))
        block_stage = ctx.enter_context(tc.tile_pool(name="block_stage", bufs=BLOCKS))
        flip_banks = ctx.enter_context(tc.psum_pool(name="flip_banks", bufs=TAP_PAIRS))
        sum_banks = ctx.enter_context(tc.psum_pool(name="sum_banks", bufs=8 - TAP_PAIRS))

        x_bands = [
            keep.tile([P, N_IMG, PACK, end - first, W], BF16, name="x_band%d" % k)
            for k, (first, end) in enumerate(LOADED_ROWS)
        ]

        def x_rows(b, n):
            first, end = band_rows(b)
            k = min(b, len(LOADED_ROWS) - 1)
            start = LOADED_ROWS[k][0]
            return x_bands[k][:, n, :, first - start : end - start, :]

        g_raw = keep.tile([P, FLIPPED, G_ROW], BF16)
        g_chunks = [keep.tile([P, G_ROW // CHUNKS], BF16, name="g_chunk%d" % h) for h in range(CHUNKS)]
        g_left = keep.tile([P, G_ROW], BF16)
        g_ordered = [
            [keep.tile([P, KW, HALVES, P, 2], BF16, name="g_ordered%d_%d" % (a, kh)) for kh in range(KH)]
            for a in range(FLIPPED)
        ]
        g_pieces = keep.tile([P, P, PIECE_PITCH], BF16)
        identity = keep.tile([P, P], F32)
        x_codes = keep.tile([P, KW, H * ROW_COLS], U32, align_bytes=64)
        x_scales = keep.tile([P, KW, H * ROW_COLS], U8, align_bytes=64)
        x_extra = keep.tile([P, STEPS, EXTRA_PIXELS, PACK], BF16, align_bytes=64)
        extra_codes = keep.tile([P, STEPS, EXTRA_PIXELS], U32, align_bytes=64)
        extra_scales = keep.tile([P, STEPS, EXTRA_PIXELS], U8, align_bytes=64)
        g_codes = keep.tile([P, TAPS, STEPS, P], U32, align_bytes=64)
        g_scales = keep.tile([P, TAPS, STEPS, P], U8, align_bytes=64)

        idle_operand = keep.tile([P, N_COLS], BF16)
        nc.vector.memset(idle_operand[:], 0.0)
        scratch = keep.tile([P, 1], BF16)
        nc.scalar.copy(out=scratch[:], in_=idle_operand[:, 0:1])
        make_identity(nc, identity[:])
        nc.vector.memset(x_extra[:], 0.0)
        odd_left = g_left[:].rearrange("o (q e) -> o q e", e=2 * TAPS)
        nc.vector.memset(odd_left[:, :, 2 * TAPS - 2 : 2 * TAPS], 0.0)
        g_rows = g.rearrange("o c kh kw -> o (c kh kw)")
        def load_band(s):
            first, end = LOADED_ROWS[s]
            for n in range(N_IMG):
                nc.sync.dma_start(
                    out=x_bands[s][:, n, :, :, :].rearrange("p t r c -> p t (r c)"),
                    in_=x[n, :, first:end, :].rearrange("(p t) r c -> p t (r c)", t=PACK),
                )

        def load_tile(s):
            nc.sync.dma_start(out=g_raw[:, s, :], in_=g_rows[s * P : (s + 1) * P, :])

        for h in range(CHUNKS):
            cols = slice(h * G_ROW // CHUNKS, (h + 1) * G_ROW // CHUNKS)
            nc.sync.dma_start(out=g_chunks[h][:], in_=g_rows[0:P, cols])
        load_band(0)
        load_band(1)
        load_tile(1)
        load_band(2)
        load_tile(2)
        for half in range(2):
            first_o = FLIPPED * P + half * HALF
            nc.sync.dma_start(
                out=g_pieces[:, half * HALF : (half + 1) * HALF, 0:PIECE],
                in_=g_rows[first_o : first_o + HALF, :].rearrange("o (p e) -> p o e", e=PIECE),
            )

        def group_rows(b, n, r0, r1, x_grouped, copy):
            copy(
                out=x_grouped[:, r0:r1, n, :, :].rearrange("p r (c i) t -> p r c t i", i=4),
                in_=x_rows(b, n)[:, :, r0:r1, 0:WO].rearrange("p t r (c i) -> p r c t i", i=4),
            )

        def group_image(b, n, x_grouped, copy):
            first, end = band_rows(b)
            group_rows(b, n, 0, end - first, x_grouped, copy)

        def group_extra(b, copy):
            first, end = band_rows(b)
            count = end - first
            extra = x_extra[:, b, 0 : count * N_IMG * EXTRA, :].rearrange("p (r n c) t -> p r n c t", n=N_IMG, c=EXTRA)
            for n in range(N_IMG):
                copy(
                    out=extra[:, :, n, :, :], in_=x_rows(b, n)[:, :, :, WO:W].rearrange("p t r c -> p r c t")
                )

        def quantise_x(b, x_grouped):
            first, end = band_rows(b)
            count = end - first
            r = 0
            while r < count:
                rows = QUANT_ROWS
                while rows > count - r:
                    rows //= 2
                cols = slice((first + r) * ROW_COLS, (first + r + rows) * ROW_COLS)
                nc.vector.quantize_mx(
                    out=x_codes[:, 0, cols].bitcast(E4M3_X4),
                    scales=x_scales[:, 0, cols],
                    in_=x_grouped[:, r : r + rows].rearrange("p r n j t -> p (r n j t)"),
                )
                r += rows
            nc.vector.quantize_mx(
                out=extra_codes[:, b, :].bitcast(E4M3_X4),
                scales=extra_scales[:, b, :],
                in_=x_extra[:, b, :, :].rearrange("p c t -> p (c t)"),
            )

        def move_x(b, kw):
            first, end = band_rows(b)
            cols = slice(first * ROW_COLS, end * ROW_COLS)
            spare = slice(0, (end - first) * N_IMG * EXTRA)
            views = [
                (x_codes[:, 0, cols].bitcast(I32), x_codes[:, kw, cols].bitcast(I32), extra_codes[:, b, spare].bitcast(I32)),
                (x_scales[:, 0, cols], x_scales[:, kw, cols], extra_scales[:, b, spare]),
            ]
            for whole, moved, extra in views:
                whole = whole.rearrange("p (q j) -> p q j", j=WO)
                moved = moved.rearrange("p (q j) -> p q j", j=WO)
                extra = extra.rearrange("p (q c) -> p q c", c=EXTRA)
                nc.vector.tensor_copy(out=moved[:, :, 0 : WO - kw], in_=whole[:, :, kw:WO])
                nc.vector.tensor_copy(out=moved[:, :, WO - kw : WO], in_=extra[:, :, 0:kw])

        def new_stage():
            return x_stage.tile([P, BAND, N_IMG, WO, PACK], BF16, align_bytes=64, name="x_grouped")

        def order_channels(source, a, kh, p_range, copy):
            by_tap = source.rearrange("o (p u e k) -> o u p e k", u=HALVES, e=2, k=TAPS)
            copy(
                out=g_ordered[a][kh][:, :, :, p_range, :].rearrange("o k u p e -> o u p e k"),
                in_=by_tap[:, :, :, :, kh * KW : (kh + 1) * KW],
            )

        def order_tile(a, kh, copy):
            order_channels(g_raw[:, a, :], a, kh, slice(0, P), copy)

        def order_chunk(h, kh, copy):
            order_channels(g_chunks[h][:], 0, kh, slice(h * CHUNK_P, (h + 1) * CHUNK_P), copy)

        def flip_pair(a, pair, banks):
            for tap in range(2 * pair, min(2 * pair + 2, TAPS)):
                for u in range(HALVES):
                    words = g_ordered[a][tap // KW][:, tap % KW, u, :, :].rearrange("o p e -> o (p e)").bitcast(F32)
                    nc.tensor.transpose(banks[pair][:, (tap % 2) * HALVES + u, :], words, identity[:])

        def shift_odd_channels():
            odd_raw = g_raw[:, 1, :].rearrange("o (q e) -> o q e", e=2 * TAPS)
            nc.scalar.copy(out=odd_left[:, :, TAPS - 1 : 2 * TAPS - 1], in_=odd_raw[:, :, TAPS : 2 * TAPS])

        def flip_channels(parity, banks):
            source = g_raw[:, 1, :] if parity == 0 else g_left[:]
            words = source.bitcast(F32).rearrange("o (p w) -> o w p", w=WORDS)
            for pair in range(TAP_PAIRS):
                for t in range(parity, PACK, 2):
                    first_word = (t * TAPS) // 2
                    nc.tensor.transpose(banks[pair][:, t, :], words[:, first_word + pair, :], identity[:])

        def empty_bank(pair, banks, copy):
            taps = min(2, TAPS - 2 * pair)
            g_grouped = g_stage.tile([P, 2, P, PACK], BF16, align_bytes=64)
            halves = banks[pair][:].bitcast(BF16).rearrange("p t (o h) -> p h o t", h=2)
            copy(out=g_grouped[:, 0:taps, :, :], in_=halves[:, 0:taps, :, :])
            return g_grouped

        def flip_tile(a, banks):
            for pair in range(TAP_PAIRS):
                flip_pair(a, pair, banks)

        def empty_taps(taps, banks, copy):
            count = taps.stop - taps.start
            pair = taps.start // 2
            g_grouped = g_stage.tile([P, 2, P, PACK], BF16, align_bytes=64)
            by_word = banks[pair][:].rearrange("p (k u) o -> p k o u", u=HALVES)
            in_bank = slice(taps.start - 2 * pair, taps.stop - 2 * pair)
            copy(out=g_grouped[:, 0:count, :, :].bitcast(F32), in_=by_word[:, in_bank, :, :])
            return g_grouped

        def quantise_taps(a, taps, g_grouped):
            for k, tap in enumerate(range(taps.start, taps.stop)):
                nc.vector.quantize_mx(
                    out=g_codes[:, tap, a, :].bitcast(E5M2_X4),
                    scales=g_scales[:, tap, a, :],
                    in_=g_grouped[:, k, :, :].rearrange("p o t -> p (o t)"),
                )

        def quantise_tile_in_pieces():
            for half in range(2):
                o_half = slice(half * HALF, (half + 1) * HALF)
                by_tap = g_pieces[:, o_half, 0:PIECE].rearrange("p o (t k) -> p k o t", k=TAPS)
                for kh in range(KH):
                    piece_grouped = piece_stage.tile([P, KW, HALF, PACK], BF16, align_bytes=64)
                    nc.vector.tensor_copy(
                        out=piece_grouped[:].rearrange("p k o t -> p o t k"),
                        in_=by_tap[:, kh * KW : (kh + 1) * KW, :, :].rearrange("p k o t -> p o t k"),
                    )
                    for kw in range(KW):
                        nc.vector.quantize_mx(
                            out=g_codes[:, kh * KW + kw, FLIPPED, o_half].bitcast(E5M2_X4),
                            scales=g_scales[:, kh * KW + kw, FLIPPED, o_half],
                            in_=piece_grouped[:, kw, :, :].rearrange("p o t -> p (o t)"),
                        )

        def new_banks():
            return [flip_banks.tile([P, PACK, P], F32, name="flipped") for pair in range(TAP_PAIRS)]

        def one_pass(a, b, tap, sums, start, stop):
            kh, kw = divmod(tap, KW)
            first_col = (first_output_row(b) + kh) * ROW_COLS
            cols = slice(first_col, first_col + N_COLS)
            nc.tensor.matmul_mx(
                out=sums[:],
                lhsT=g_codes[:, tap, a, :].bitcast(E5M2_X4),
                lhsT_scale=g_scales[:, tap, a, :],
                rhs=x_codes[:, kw, cols].bitcast(E4M3_X4),
                rhs_scale=x_scales[:, kw, cols],
                start=start,
                stop=stop,
            )

        def block_pass(k, tap, sums, start, stop):
            kh, kw = divmod(tap, KW)
            first_col = (LAST_ROW + k * BLOCK_ROWS + kh) * ROW_COLS
            cols = slice(first_col, first_col + P)
            nc.tensor.matmul_mx(
                out=sums[:],
                lhsT=x_codes[:, kw, cols].bitcast(E4M3_X4),
                lhsT_scale=x_scales[:, kw, cols],
                rhs=g_codes[:, tap, :, :].rearrange("p a o -> p (a o)").bitcast(E5M2_X4),
                rhs_scale=g_scales[:, tap, :, :].rearrange("p a o -> p (a o)"),
                start=start,
                stop=stop,
            )

        def idle_matmuls(count):
            sums = sum_banks.tile([P, N_COLS], F32)
            for unused in range(count):
                nc.tensor.matmul(sums[:], lhsT=idle_operand[:, 0:P], rhs=idle_operand[:], start=True, stop=True)

        def store_product(a, b, sums):
            result = out_stage.tile([P, N_IMG, ROWS, WO], F32)
            nc.scalar.copy(out=result[:], in_=sums[:].rearrange("p (i n j) -> p n i j", n=N_IMG, j=WO))
            queue = nc.sync if a < STEPS - 1 else nc.scalar
            queue.dma_start(
                out=out[:, a * P : (a + 1) * P, b * ROWS : (b + 1) * ROWS, :].rearrange("n o i j -> o n (i j)"),
                in_=result[:].rearrange("p n i j -> p n (i j)"),
            )

        ctx.enter_context(tc.manual_schedule())
        by_vector, by_scalar = nc.vector.tensor_copy, nc.scalar.copy

        def pair_taps(pair):
            return slice(2 * pair, min(2 * pair + 2, TAPS))

        for h in range(CHUNKS):
            order_chunk(h, 0, by_vector)
            order_chunk(h, 2, by_scalar)
            order_chunk(h, 1, by_vector)
        idle_matmuls(EARLY_MATMULS)
        banks = new_banks()
        flip_tile(0, banks)
        idle_matmuls(LATE_MATMULS)

        x_grouped = new_stage()
        group_rows(0, 0, 0, BAND, x_grouped, by_vector)
        pair_0 = empty_taps(pair_taps(0), banks, by_scalar)
        group_rows(0, 1, 4, BAND, x_grouped, by_scalar)
        group_rows(0, 1, 0, 4, x_grouped, by_vector)
        group_extra(0, by_scalar)
        quantise_taps(0, pair_taps(0), pair_0)
        pair_1 = empty_taps(pair_taps(1), banks, by_scalar)
        quantise_x(0, x_grouped)
        pair_3 = empty_taps(pair_taps(3), banks, by_scalar)
        quantise_taps(0, pair_taps(1), pair_1)
        move_x(0, 1)
        pair_2 = empty_taps(pair_taps(2), banks, by_scalar)
        quantise_taps(0, pair_taps(3), pair_3)
        pair_4 = empty_taps(pair_taps(4), banks, by_scalar)
        quantise_taps(0, pair_taps(2), pair_2)
        move_x(0, 2)
        quantise_taps(0, pair_taps(4), pair_4)

        x_grouped = new_stage()
        group_image(1, 0, x_grouped, by_vector)
        group_image(1, 1, x_grouped, by_scalar)
        group_extra(1, by_vector)
        shift_odd_channels()
        quantise_x(1, x_grouped)
        move_x(1, 1)
        move_x(1, 2)

        by_kw = [kh * KW + kw for kw in range(KW) for kh in range(KH)]
        first_order = [0, 3, 6, 1, 7, 4, 2, 5, 8]
        def prepare_band(b):
            x_grouped = new_stage()
            group_image(b, 0, x_grouped, by_vector)
            group_image(b, 1, x_grouped, by_scalar)
            group_extra(b, by_vector)
            quantise_x(b, x_grouped)
            move_x(b, 1)
            move_x(b, 2)

        sequence = [(0, 0), (0, 1), (1, 0), (1, 1), (0, 2), (1, 2), (2, 0), (2, 1), (2, 2)]
        for i, (a, b) in enumerate(sequence):
            sums = sum_banks.tile([P, N_COLS], F32)
            order = first_order if i == 0 else by_kw if a == 0 else list(range(TAPS))
            for j, tap in enumerate(order):
                one_pass(a, b, tap, sums, j == 0, j == TAPS - 1)
                if i == 0 and j == 1:
                    banks = new_banks()
                    flip_channels(0, banks)
                if i == 1 and j == 1:
                    flip_channels(1, banks)
            if (a, b) == (0, 2):
                banks = new_banks()
                flip_tile(2, banks)
            if i == 1:
                g0 = empty_bank(0, banks, by_scalar)
                g1 = empty_bank(1, banks, by_vector)
                quantise_taps(1, pair_taps(0), g0)
                g2 = empty_bank(2, banks, by_scalar)
                quantise_taps(1, pair_taps(1), g1)
                g3 = empty_bank(3, banks, by_vector)
                quantise_taps(1, pair_taps(2), g2)
                g4 = empty_bank(4, banks, by_scalar)
                quantise_taps(1, pair_taps(3), g3)
                quantise_taps(1, pair_taps(4), g4)
            store_product(a, b, sums)
            if i == 1:
                prepare_band(2)
                for kh in range(KH):
                    order_tile(2, kh, by_vector)
            if (a, b) == (0, 2):
                for pair in range(TAP_PAIRS):
                    g_grouped = empty_taps(pair_taps(pair), banks, by_scalar)
                    quantise_taps(2, pair_taps(pair), g_grouped)
                prepare_band(3)
                quantise_tile_in_pieces()

        sums = [flip_banks.tile([P, N_COLS], F32, name="flipped") for k in range(BLOCKS)]
        for tap in range(TAPS):
            for k in range(BLOCKS):
                block_pass(k, tap, sums[k], tap == 0, tap == TAPS - 1)
        block_sums = []
        for k in range(BLOCKS):
            pixels = block_stage.tile([P, CO], F32)
            nc.scalar.copy(out=pixels[:], in_=sums[k][:])
            block_sums.append(pixels)
        last_rows = keep.tile([P, STEPS, N_IMG, BLOCKS * BLOCK_ROWS, WO], F32)
        for b in range(STEPS - 1):
            sums = sum_banks.tile([P, N_COLS], F32)
            for tap in range(TAPS):
                one_pass(STEPS - 1, b, tap, sums, tap == 0, tap == TAPS - 1)
            if b == 0:
                banks = [flip_banks.tile([P, STEPS, P], F32, name="flipped") for k in range(BLOCKS)]
                for k in range(BLOCKS):
                    for a in range(STEPS):
                        nc.tensor.transpose(banks[k][:, a, :], block_sums[k][:, a * P : (a + 1) * P], identity[:])
            store_product(STEPS - 1, b, sums)
            if b == 0:
                for k in range(BLOCKS):
                    rows = slice(k * BLOCK_ROWS, (k + 1) * BLOCK_ROWS)
                    nc.scalar.copy(
                        out=last_rows[:, :, :, rows, :],
                        in_=banks[k][:].rearrange("p a (r n j) -> p a n r j", n=N_IMG, j=WO),
                    )
                for a in range(STEPS):
                    nc.scalar.dma_start(
                        out=out[:, a * P : (a + 1) * P, LAST_ROW:HO, :].rearrange("n o i j -> o n (i j)"),
                        in_=last_rows[:, a, :, :, :].rearrange("p n r j -> p n (r j)"),
                    )
